import numpy as np
import ml_dtypes


def mxq(x, axis, fmt="e4m3"):
    dtype, down = {"e4m3": (ml_dtypes.float8_e4m3fn, 7), "e5m2": (ml_dtypes.float8_e5m2, 14)}[fmt]
    v = np.moveaxis(np.asarray(x, np.float32).astype(ml_dtypes.bfloat16).astype(np.float64), axis, -1)
    blocks = v.reshape(v.shape[:-1] + (-1, 32))
    amax = np.abs(blocks).max(-1, keepdims=True)
    byte = np.maximum(np.where(amax > 0, np.frexp(amax)[1] - 1 + 127, 0) - down, 1)
    scale = np.exp2(byte - 127.0)
    codes = (blocks / scale).astype(np.float32).astype(dtype).astype(np.float64)
    return np.moveaxis((codes * scale).reshape(v.shape), -1, axis)


WIDE = False


def mx_kscale(k):
    if not WIDE:
        return np.ones(k)
    levels = np.array([10, -10, 5, -5, 0])
    a = np.random.permutation(np.resize(levels, k // 512 * 4)).reshape(k // 512, 4)
    idx = np.arange(k)
    return np.exp2(a[idx // 512, idx % 128 // 32])


BF16 = ml_dtypes.bfloat16


def bf(x):
    return np.asarray(x, np.float32).astype(BF16)


def f64(x):
    return np.asarray(x).astype(np.float64)


E2M1 = np.array([0.0, 0.5, 1.0, 1.5, 2.0, 3.0, 4.0, 6.0, -0.0, -0.5, -1.0, -1.5, -2.0, -3.0, -4.0, -6.0])


def pack_weight(w, fmt):
    k, n = w.shape
    w = f64(bf(w)).reshape(k // 32, 32, n)
    amax = np.abs(w).max(1)
    if fmt == "e4m3":
        byte = np.frexp(amax)[1] - 1 + 127 - 7
    else:
        mant, ex = np.frexp(amax / 6.0)
        byte = np.where(mant > 0.5, ex, ex - 1) + 127
    byte = np.clip(np.where(amax > 0, byte, 1), 1, 254)
    scaled = (w * np.exp2(127.0 - byte)[:, None, :]).reshape(k, n).astype(np.float32)
    by_word = np.ascontiguousarray(scaled.reshape(k // 512, 128, 4, n).transpose(0, 1, 3, 2))
    if fmt == "e4m3":
        words = by_word.astype(ml_dtypes.float8_e4m3fn).view(np.uint8)
    else:
        c = by_word.astype(ml_dtypes.float4_e2m1fn).view(np.uint8) & 0xF
        words = c[..., 0::2] | (c[..., 1::2] << 4)
    return np.ascontiguousarray(words), np.ascontiguousarray(byte.astype(np.uint8).reshape(k // 512, 16, n))


def unpack_weight(words, scales, fmt):
    g, p, n, _ = words.shape
    if fmt == "e4m3":
        vals = np.ascontiguousarray(words).view(ml_dtypes.float8_e4m3fn).astype(np.float64)
    else:
        nib = np.empty((g, p, n, 4), np.uint8)
        nib[..., 0::2] = words & 0xF
        nib[..., 1::2] = words >> 4
        vals = E2M1[nib]
    vals = vals * np.repeat(np.exp2(scales.astype(np.float64) - 127.0), 8, axis=1)[..., None]
    return vals.transpose(0, 1, 3, 2).reshape(g * 512, n)

def pack4(w):
    words, scales = pack_weight(w, "e2m1")
    return words.reshape(words.shape[0], 128, -1), scales


def unpack4(words, scales):
    return unpack_weight(words.reshape(words.shape[0], 128, -1, 2), scales, "e2m1")


B, S, E, N_HEAD, MP_NUM, ROTARY_DIM = 2, 2048, 512, 4, 4, 64
HEAD_DIM = E // N_HEAD
LOCAL = E // MP_NUM
ROPE_BASE = 10000.0


def rotate_every_two(x):
    x1 = x[..., 0::2]
    x2 = x[..., 1::2]
    return np.stack((-x2, x1), axis=-1).reshape(x.shape)


def rope(x, sin, cos):
    x_rot = x[..., :ROTARY_DIM]
    x_pass = x[..., ROTARY_DIM:]
    x_rot = x_rot * cos + rotate_every_two(x_rot) * sin
    return np.concatenate([x_rot, x_pass], axis=-1)


def setup_inputs():
    s = mx_kscale(E)
    hidden_states = bf(np.random.standard_normal((B, S, E)) * s)
    w = np.random.standard_normal((3 * E, E)) / np.sqrt(E) / s[None, :]
    words, scales = pack4(w.T)
    return {"hidden_states": hidden_states,
            "w_qkv_words": words,
            "w_qkv_scales": scales}


def reference(hidden_states, w_qkv_words, w_qkv_scales):
    qkv = mxq(f64(hidden_states), 2, "e4m3") @ unpack4(w_qkv_words, w_qkv_scales)
    qkv = qkv.reshape(B, S, MP_NUM, 3 * LOCAL)
    q = qkv[..., :LOCAL].reshape(B, S, N_HEAD, HEAD_DIM)
    v = qkv[..., LOCAL:2 * LOCAL].reshape(B, S, N_HEAD, HEAD_DIM)
    k = qkv[..., 2 * LOCAL:].reshape(B, S, N_HEAD, HEAD_DIM)
    inv_freq = 1.0 / (ROPE_BASE ** (np.arange(0, ROTARY_DIM, 2) / ROTARY_DIM))
    freqs = np.arange(S)[:, None] * inv_freq[None, :]
    sin = np.repeat(np.sin(freqs), 2, axis=-1)[None, :, None, :]
    cos = np.repeat(np.cos(freqs), 2, axis=-1)[None, :, None, :]
    q = rope(q, sin, cos)
    k = rope(k, sin, cos)
    return q.transpose(0, 2, 1, 3), k.transpose(0, 2, 1, 3), v.transpose(0, 2, 1, 3)

@@ -1,0 +1,280 @@
+import math
+from contextlib import ExitStack
+
+import concourse.mybir as mybir
+from concourse.masks import make_identity
+
+F32 = mybir.dt.float32
+BF16 = mybir.dt.bfloat16
+I32 = mybir.dt.int32
+U32 = mybir.dt.uint32
+U8 = mybir.dt.uint8
+FP8X4 = mybir.dt.float8_e4m3fn_x4
+FP4X4 = mybir.dt.float4_e2m1fn_x4
+ALU = mybir.AluOpType
+FUNC = mybir.ActivationFunctionType
+
+P = 128
+BATCH, SEQ, EMBED = 2, 2048, 512
+HEADS, HEAD_DIM, ROTARY = 4, 128, 64
+PAIRS = ROTARY // 2
+ROPE_BASE = 10000.0
+
+ROWS = 8
+CHUNK = P * ROWS
+HALVES = SEQ // CHUNK
+CHUNKS = BATCH * HALVES
+
+GROUP = 512
+VALUES, PASSED, ROTATED = 0, 1, 2
+QUERY, VALUE, KEY = 0, 1, 2
+
+ROUND = 1.5 * 2.0**23
+
+FLOPS = 2 * BATCH * SEQ * EMBED * 3 * EMBED
+
+
+def tile_ttcodegenattention_pa_t_kernel(
+    tc, hidden_states, w_qkv_words, w_qkv_scales, out_0, out_1, out_2
+):
+    nc = tc.nc
+    with ExitStack() as ctx:
+        consts = ctx.enter_context(tc.tile_pool(name="consts", bufs=1))
+        angle_pool = ctx.enter_context(tc.tile_pool(name="angles", bufs=2))
+        x_pool = ctx.enter_context(tc.tile_pool(name="x", bufs=CHUNKS))
+        quant_pool = ctx.enter_context(tc.tile_pool(name="quant", bufs=2))
+        prod_pool = ctx.enter_context(tc.tile_pool(name="prod", bufs=3))
+        stage_pool = ctx.enter_context(tc.tile_pool(name="stage", bufs=2))
+        psum_x = ctx.enter_context(tc.psum_pool(name="psum_x", bufs=2))
+        psum_copy = ctx.enter_context(tc.psum_pool(name="psum_copy", bufs=3))
+        psum_rope = ctx.enter_context(tc.psum_pool(name="psum_rope", bufs=3))
+
+        x_tiles = []
+        for n in range(CHUNKS):
+            x_tiles.append(x_pool.tile([P, ROWS, EMBED], BF16, name="x_chunk"))
+
+        def load_x(n, j0, j1):
+            b, c = divmod(n, HALVES)
+            rows = hidden_states[b, c * CHUNK : (c + 1) * CHUNK, :]
+            nc.sync.dma_start(
+                out=x_tiles[n][:, j0:j1, :],
+                in_=rows.rearrange("(p j) k -> p j k", j=ROWS)[:, j0:j1, :],
+            )
+
+        load_x(0, 0, ROWS // 2)
+        load_x(0, ROWS // 2, ROWS)
+
+        raw_planes = consts.tile([P, 3 * GROUP], U8, align_bytes=64)
+        nc.vector.memset(raw_planes[:].bitcast(I32), 0)
+        scale_rows = w_qkv_scales[0].bitcast(I32)
+        for quadrant in range(4):
+            nc.sync.dma_start(
+                out=raw_planes[32 * quadrant : 32 * quadrant + 4, :].bitcast(I32),
+                in_=scale_rows[4 * quadrant : 4 * quadrant + 4, :],
+            )
+
+        w_words = consts.tile([P, 3, 2 * GROUP], U8, align_bytes=64)
+        words_sb = w_words[:].bitcast(I32)
+        words_in = w_qkv_words[0].bitcast(I32).rearrange("p (h t c) -> p h t c", h=HEADS, t=3)
+        half = HEAD_DIM // 4
+
+        def load_words(group, side, block, first):
+            width = words_sb.shape[2] // 2
+            nc.sync.dma_start(
+                out=words_sb[:, group, side * width : (side + 1) * width].rearrange(
+                    "p (h c) -> p h c", h=HEADS
+                ),
+                in_=words_in[:, :, block, first : first + half],
+            )
+
+        nc.sync.dma_start(
+            out=words_sb[:, VALUES, :].rearrange("p (h c) -> p h c", h=HEADS),
+            in_=words_in[:, :, VALUE, :],
+        )
+        load_words(ROTATED, 0, QUERY, 0)
+        load_words(ROTATED, 1, KEY, 0)
+        load_words(PASSED, 0, QUERY, half)
+        load_words(PASSED, 1, KEY, half)
+        for n in range(1, CHUNKS):
+            load_x(n, 0, ROWS)
+
+        w_planes = consts.tile([P, 3, GROUP], U8, align_bytes=64)
+        planes_sb = w_planes[:].bitcast(I32)
+        planes_in = raw_planes[:].bitcast(I32).rearrange("p (h t c) -> p h t c", h=HEADS, t=3)
+        quarter = HEAD_DIM // 8
+        nc.vector.tensor_copy(
+            out=planes_sb[:, VALUES, :].rearrange("p (h c) -> p h c", h=HEADS),
+            in_=planes_in[:, :, VALUE, :],
+        )
+        for group, first in ((ROTATED, 0), (PASSED, quarter)):
+            nc.vector.tensor_copy(
+                out=planes_sb[:, group, :].rearrange("p (t h c) -> p t h c", t=2, h=HEADS),
+                in_=planes_in[:, :, QUERY : KEY + 1 : 2, first : first + quarter].rearrange(
+                    "p h t c -> p t h c"
+                ),
+            )
+
+        ident = consts.tile([P, P], F32)
+        make_identity(nc, ident[:])
+
+        position_int = consts.tile([P, HALVES, ROWS], I32)
+        nc.gpsimd.iota(
+            position_int[:], pattern=[[CHUNK, HALVES], [1, ROWS]], base=0, channel_multiplier=ROWS
+        )
+        position = consts.tile([P, HALVES, ROWS], F32)
+        nc.vector.tensor_copy(out=position[:], in_=position_int[:])
+        ratio = ROPE_BASE ** (-1.0 / PAIRS)
+        frequency = consts.tile([P, PAIRS], F32)
+        nc.vector.memset(frequency[:, 0:1], 1.0)
+        nc.vector.tensor_scalar_mul(
+            out=frequency[:, 0:1], in0=frequency[:, 0:1], scalar1=1.0 / (2.0 * math.pi)
+        )
+        filled = 1
+        while filled < PAIRS:
+            nc.vector.tensor_scalar_mul(
+                out=frequency[:, filled : 2 * filled],
+                in0=frequency[:, 0:filled],
+                scalar1=ratio**filled,
+            )
+            filled *= 2
+
+        table = consts.tile([P, 4, HALVES, ROWS, PAIRS], F32)
+        shape = [P, ROWS, PAIRS]
+        for c in range(HALVES):
+            turns = angle_pool.tile(shape, F32)
+            nc.vector.tensor_tensor(
+                out=turns[:],
+                in0=position[:, c, :].unsqueeze(2).to_broadcast(shape),
+                in1=frequency[:].unsqueeze(1).to_broadcast(shape),
+                op=ALU.mult,
+            )
+            whole = angle_pool.tile(shape, F32)
+            nc.vector.tensor_scalar_add(out=whole[:], in0=turns[:], scalar1=ROUND)
+            part = angle_pool.tile([P, 2, ROWS, PAIRS], F32)
+            nc.vector.scalar_tensor_tensor(
+                out=part[:, 0],
+                in0=whole[:],
+                scalar=ROUND,
+                in1=turns[:],
+                op0=ALU.subtract,
+                op1=ALU.subtract,
+            )
+            nc.vector.tensor_scalar_add(out=part[:, 1], in0=part[:, 0], scalar1=0.25)
+            half_sin = angle_pool.tile([P, 2, ROWS, PAIRS], F32)
+            nc.scalar.activation(out=half_sin[:], in_=part[:], func=FUNC.Sin, scale=math.pi)
+            squared = angle_pool.tile([P, 2, ROWS, PAIRS], F32)
+            nc.scalar.activation(out=squared[:], in_=half_sin[:], func=FUNC.Square)
+            nc.gpsimd.tensor_scalar(
+                out=table[:, 0:4:3, c],
+                in0=squared[:, 0:1].to_broadcast([P, 2, ROWS, PAIRS]),
+                scalar1=-2.0,
+                scalar2=1.0,
+                op0=ALU.mult,
+                op1=ALU.add,
+            )
+            nc.gpsimd.tensor_scalar(
+                out=table[:, 2, c], in0=squared[:, 1], scalar1=-2.0, scalar2=1.0,
+                op0=ALU.mult, op1=ALU.add,
+            )
+            nc.gpsimd.tensor_scalar(
+                out=table[:, 1, c], in0=squared[:, 1], scalar1=2.0, scalar2=-1.0,
+                op0=ALU.mult, op1=ALU.add,
+            )
+
+        def quantise_chunk(n):
+            x_words = x_tiles[n][:].bitcast(F32)
+            grouped = quant_pool.tile([P, ROWS, P, 4], BF16, align_bytes=64)
+            grouped_words = grouped[:].bitcast(F32)
+            codes = quant_pool.tile([P, ROWS, P], U32, align_bytes=64)
+            scales = quant_pool.tile([P, ROWS, P], U8, align_bytes=64)
+            for j in range(0, ROWS, 2):
+                flipped = psum_x.tile([P, 2, 2, P], F32)
+                for a in range(2):
+                    for u in range(2):
+                        nc.tensor.transpose(
+                            flipped[:, a, u, :], x_words[:, j + a, u : EMBED // 2 : 2], ident[:]
+                        )
+                nc.scalar.copy(
+                    out=grouped_words[:, j : j + 2],
+                    in_=flipped[:].rearrange("p a u r -> p a r u"),
+                )
+            for j in range(0, ROWS, 4):
+                nc.vector.quantize_mx(
+                    out=codes[:, j : j + 4].rearrange("p j r -> p (j r)").bitcast(FP8X4),
+                    scales=scales[:, j : j + 4].rearrange("p j r -> p (j r)"),
+                    in_=grouped[:, j : j + 4].rearrange("p j r t -> p (j r t)"),
+                )
+            return codes, scales
+
+        def project_chunk(n, codes, scales):
+            b, c = divmod(n, HALVES)
+            first = c * CHUNK
+
+            def multiply(bank, group, j):
+                nc.tensor.matmul_mx(
+                    out=bank[:],
+                    lhsT=codes[:, j, :].bitcast(FP8X4),
+                    lhsT_scale=scales[:, j, :],
+                    rhs=w_words[:, group, :].bitcast(FP4X4),
+                    rhs_scale=w_planes[:, group, :],
+                    start=True,
+                    stop=True,
+                )
+
+            def store(out, staged):
+                nc.sync.dma_start(
+                    out=out[b, :, first : first + CHUNK, :].rearrange(
+                        "h (p j) d -> p h (j d)", j=ROWS
+                    ),
+                    in_=staged.rearrange("p h j d -> p h (j d)"),
+                )
+
+            stage_qk = stage_pool.tile([P, 2 * HEADS, ROWS, HEAD_DIM], F32)
+            stage_v = stage_pool.tile([P, HEADS, ROWS, HEAD_DIM], F32)
+            for j in range(ROWS):
+                for a in (2 * j, 2 * j + 1):
+                    group, row = divmod(a, ROWS)
+                    bank = psum_copy.tile([P, GROUP], F32)
+                    multiply(bank, group, row)
+                    if group == VALUES:
+                        nc.scalar.copy(
+                            out=stage_v[:, :, row, :],
+                            in_=bank[:].rearrange("p (h d) -> p h d", h=HEADS),
+                        )
+                    else:
+                        nc.scalar.copy(
+                            out=stage_qk[:, :, row, ROTARY:],
+                            in_=bank[:].rearrange("p (g d) -> p g d", g=2 * HEADS),
+                        )
+                    if a == ROWS - 1:
+                        store(out_2, stage_v[:])
+                rope = psum_rope.tile([P, GROUP], F32)
+                multiply(rope, ROTATED, j)
+                full = [P, 2, 2, 2 * HEADS, PAIRS]
+                prod = prod_pool.tile(full, F32)
+                nc.vector.tensor_tensor(
+                    out=prod[:],
+                    in0=rope[:]
+                    .rearrange("p (g i m) -> p m g i", g=2 * HEADS, m=2)
+                    .unsqueeze(1)
+                    .to_broadcast(full),
+                    in1=table[:, :, c, j, :]
+                    .rearrange("p (e m) i -> p e m i", e=2)
+                    .unsqueeze(3)
+                    .to_broadcast(full),
+                    op=ALU.mult,
+                )
+                nc.gpsimd.tensor_tensor(
+                    out=stage_qk[:, :, j, 0:ROTARY].rearrange("p g (i e) -> p g i e", e=2),
+                    in0=prod[:, :, 0].rearrange("p e g i -> p g i e"),
+                    in1=prod[:, :, 1].rearrange("p e g i -> p g i e"),
+                    op=ALU.add,
+                )
+            store(out_0, stage_qk[:, 0:HEADS])
+            store(out_1, stage_qk[:, HEADS : 2 * HEADS])
+
+        quantised = quantise_chunk(0)
+        for n in range(CHUNKS):
+            following = quantise_chunk(n + 1) if n + 1 < CHUNKS else None
+            project_chunk(n, quantised[0], quantised[1])
+            quantised = following

@@ -138,7 +138,7 @@ def tile_ttcodegenattention_pa_t_kernel(
             )
             filled *= 2
 
-        table = consts.tile([P, 4, HALVES, ROWS, PAIRS], F32)
+        table = consts.tile([P, 2, HALVES, ROWS, PAIRS, 2], F32)
         shape = [P, ROWS, PAIRS]
         for c in range(HALVES):
             turns = angle_pool.tile(shape, F32)
@@ -164,22 +164,15 @@ def tile_ttcodegenattention_pa_t_kernel(
             nc.scalar.activation(out=half_sin[:], in_=part[:], func=FUNC.Sin, scale=math.pi)
             squared = angle_pool.tile([P, 2, ROWS, PAIRS], F32)
             nc.scalar.activation(out=squared[:], in_=half_sin[:], func=FUNC.Square)
-            nc.gpsimd.tensor_scalar(
-                out=table[:, 0:4:3, c],
-                in0=squared[:, 0:1].to_broadcast([P, 2, ROWS, PAIRS]),
-                scalar1=-2.0,
-                scalar2=1.0,
-                op0=ALU.mult,
-                op1=ALU.add,
-            )
-            nc.gpsimd.tensor_scalar(
-                out=table[:, 2, c], in0=squared[:, 1], scalar1=-2.0, scalar2=1.0,
-                op0=ALU.mult, op1=ALU.add,
-            )
-            nc.gpsimd.tensor_scalar(
-                out=table[:, 1, c], in0=squared[:, 1], scalar1=2.0, scalar2=-1.0,
-                op0=ALU.mult, op1=ALU.add,
-            )
+            for m, e, phase, sign in ((0, 0, 0, 1.0), (1, 1, 0, 1.0), (0, 1, 1, 1.0), (1, 0, 1, -1.0)):
+                nc.gpsimd.tensor_scalar(
+                    out=table[:, m, c, :, :, e],
+                    in0=squared[:, phase],
+                    scalar1=-2.0 * sign,
+                    scalar2=sign,
+                    op0=ALU.mult,
+                    op1=ALU.add,
+                )
 
         def quantise_chunk(n):
             x_words = x_tiles[n][:].bitcast(F32)
@@ -250,24 +243,21 @@ def tile_ttcodegenattention_pa_t_kernel(
                         store(out_2, stage_v[:])
                 rope = psum_rope.tile([P, GROUP], F32)
                 multiply(rope, ROTATED, j)
-                full = [P, 2, 2, 2 * HEADS, PAIRS]
+                full = [P, 2, 2 * HEADS, PAIRS, 2]
                 prod = prod_pool.tile(full, F32)
                 nc.vector.tensor_tensor(
                     out=prod[:],
                     in0=rope[:]
                     .rearrange("p (g i m) -> p m g i", g=2 * HEADS, m=2)
-                    .unsqueeze(1)
+                    .unsqueeze(4)
                     .to_broadcast(full),
-                    in1=table[:, :, c, j, :]
-                    .rearrange("p (e m) i -> p e m i", e=2)
-                    .unsqueeze(3)
-                    .to_broadcast(full),
+                    in1=table[:, :, c, j].unsqueeze(2).to_broadcast(full),
                     op=ALU.mult,
                 )
                 nc.gpsimd.tensor_tensor(
-                    out=stage_qk[:, :, j, 0:ROTARY].rearrange("p g (i e) -> p g i e", e=2),
-                    in0=prod[:, :, 0].rearrange("p e g i -> p g i e"),
-                    in1=prod[:, :, 1].rearrange("p e g i -> p g i e"),
+                    out=stage_qk[:, :, j, 0:ROTARY],
+                    in0=prod[:, 0].rearrange("p g i e -> p g (i e)"),
+                    in1=prod[:, 1].rearrange("p g i e -> p g (i e)"),
                     op=ALU.add,
                 )
             store(out_0, stage_qk[:, 0:HEADS])

@@ -48,6 +48,7 @@ def tile_ttcodegenattention_pa_t_kernel(
         psum_x = ctx.enter_context(tc.psum_pool(name="psum_x", bufs=2))
         psum_copy = ctx.enter_context(tc.psum_pool(name="psum_copy", bufs=3))
         psum_rope = ctx.enter_context(tc.psum_pool(name="psum_rope", bufs=3))
+        ctx.enter_context(tc.manual_schedule())
 
         x_tiles = []
         for n in range(CHUNKS):
@@ -98,29 +99,12 @@ def tile_ttcodegenattention_pa_t_kernel(
         for n in range(1, CHUNKS):
             load_x(n, 0, ROWS)
 
-        w_planes = consts.tile([P, 3, GROUP], U8, align_bytes=64)
-        planes_sb = w_planes[:].bitcast(I32)
-        planes_in = raw_planes[:].bitcast(I32).rearrange("p (h t c) -> p h t c", h=HEADS, t=3)
-        quarter = HEAD_DIM // 8
-        nc.vector.tensor_copy(
-            out=planes_sb[:, VALUES, :].rearrange("p (h c) -> p h c", h=HEADS),
-            in_=planes_in[:, :, VALUE, :],
-        )
-        for group, first in ((ROTATED, 0), (PASSED, quarter)):
-            nc.vector.tensor_copy(
-                out=planes_sb[:, group, :].rearrange("p (t h c) -> p t h c", t=2, h=HEADS),
-                in_=planes_in[:, :, QUERY : KEY + 1 : 2, first : first + quarter].rearrange(
-                    "p h t c -> p t h c"
-                ),
-            )
-
-        ident = consts.tile([P, P], F32)
-        make_identity(nc, ident[:])
-
         position_int = consts.tile([P, HALVES, ROWS], I32)
         nc.gpsimd.iota(
             position_int[:], pattern=[[CHUNK, HALVES], [1, ROWS]], base=0, channel_multiplier=ROWS
         )
+        ident = consts.tile([P, P], F32)
+        make_identity(nc, ident[:])
         position = consts.tile([P, HALVES, ROWS], F32)
         nc.vector.tensor_copy(out=position[:], in_=position_int[:])
         ratio = ROPE_BASE ** (-1.0 / PAIRS)
@@ -139,8 +123,9 @@ def tile_ttcodegenattention_pa_t_kernel(
             filled *= 2
 
         table = consts.tile([P, 2, HALVES, ROWS, PAIRS, 2], F32)
-        shape = [P, ROWS, PAIRS]
-        for c in range(HALVES):
+
+        def half_angle_squares(c):
+            shape = [P, ROWS, PAIRS]
             turns = angle_pool.tile(shape, F32)
             nc.vector.tensor_tensor(
                 out=turns[:],
@@ -164,8 +149,16 @@ def tile_ttcodegenattention_pa_t_kernel(
             nc.scalar.activation(out=half_sin[:], in_=part[:], func=FUNC.Sin, scale=math.pi)
             squared = angle_pool.tile([P, 2, ROWS, PAIRS], F32)
             nc.scalar.activation(out=squared[:], in_=half_sin[:], func=FUNC.Square)
-            for m, e, phase, sign in ((0, 0, 0, 1.0), (1, 1, 0, 1.0), (0, 1, 1, 1.0), (1, 0, 1, -1.0)):
-                nc.gpsimd.tensor_scalar(
+            return squared
+
+        def fill_table(c, squared):
+            for engine, m, e, phase, sign in (
+                (nc.vector, 0, 0, 0, 1.0),
+                (nc.vector, 0, 1, 1, 1.0),
+                (nc.gpsimd, 1, 0, 1, -1.0),
+                (nc.gpsimd, 1, 1, 0, 1.0),
+            ):
+                engine.tensor_scalar(
                     out=table[:, m, c, :, :, e],
                     in0=squared[:, phase],
                     scalar1=-2.0 * sign,
@@ -174,34 +167,65 @@ def tile_ttcodegenattention_pa_t_kernel(
                     op1=ALU.add,
                 )
 
-        def quantise_chunk(n):
-            x_words = x_tiles[n][:].bitcast(F32)
+        def new_operand():
             grouped = quant_pool.tile([P, ROWS, P, 4], BF16, align_bytes=64)
-            grouped_words = grouped[:].bitcast(F32)
             codes = quant_pool.tile([P, ROWS, P], U32, align_bytes=64)
             scales = quant_pool.tile([P, ROWS, P], U8, align_bytes=64)
-            for j in range(0, ROWS, 2):
-                flipped = psum_x.tile([P, 2, 2, P], F32)
-                for a in range(2):
-                    for u in range(2):
-                        nc.tensor.transpose(
-                            flipped[:, a, u, :], x_words[:, j + a, u : EMBED // 2 : 2], ident[:]
-                        )
-                nc.scalar.copy(
-                    out=grouped_words[:, j : j + 2],
-                    in_=flipped[:].rearrange("p a u r -> p a r u"),
-                )
-            for j in range(0, ROWS, 4):
-                nc.vector.quantize_mx(
-                    out=codes[:, j : j + 4].rearrange("p j r -> p (j r)").bitcast(FP8X4),
-                    scales=scales[:, j : j + 4].rearrange("p j r -> p (j r)"),
-                    in_=grouped[:, j : j + 4].rearrange("p j r t -> p (j r t)"),
-                )
-            return codes, scales
+            return grouped, codes, scales
 
-        def project_chunk(n, codes, scales):
+        def flip_rows(n, j, operand):
+            x_words = x_tiles[n][:].bitcast(F32)
+            grouped_words = operand[0][:].bitcast(F32)
+            flipped = psum_x.tile([P, 2, 2, P], F32)
+            for a in range(2):
+                for u in range(2):
+                    nc.tensor.transpose(
+                        flipped[:, a, u, :], x_words[:, j + a, u : EMBED // 2 : 2], ident[:]
+                    )
+            nc.scalar.copy(
+                out=grouped_words[:, j : j + 2], in_=flipped[:].rearrange("p a u r -> p a r u")
+            )
+
+        def quantise_rows(j0, j1, operand):
+            grouped, codes, scales = operand
+            nc.vector.quantize_mx(
+                out=codes[:, j0:j1].rearrange("p j r -> p (j r)").bitcast(FP8X4),
+                scales=scales[:, j0:j1].rearrange("p j r -> p (j r)"),
+                in_=grouped[:, j0:j1].rearrange("p j r t -> p (j r t)"),
+            )
+
+        squared = half_angle_squares(0)
+        operand = new_operand()
+        for j in range(0, ROWS, 2):
+            flip_rows(0, j, operand)
+        fill_table(0, squared)
+
+        w_planes = consts.tile([P, 3, GROUP], U8, align_bytes=64)
+        planes_sb = w_planes[:].bitcast(I32)
+        planes_in = raw_planes[:].bitcast(I32).rearrange("p (h t c) -> p h t c", h=HEADS, t=3)
+        quarter = HEAD_DIM // 8
+        nc.vector.tensor_copy(
+            out=planes_sb[:, VALUES, :].rearrange("p (h c) -> p h c", h=HEADS),
+            in_=planes_in[:, :, VALUE, :],
+        )
+        for group, first in ((ROTATED, 0), (PASSED, quarter)):
+            nc.vector.tensor_copy(
+                out=planes_sb[:, group, :].rearrange("p (t h c) -> p t h c", t=2, h=HEADS),
+                in_=planes_in[:, :, QUERY : KEY + 1 : 2, first : first + quarter].rearrange(
+                    "p h t c -> p t h c"
+                ),
+            )
+
+        quantise_rows(0, ROWS // 2, operand)
+        quantise_rows(ROWS // 2, ROWS, operand)
+
+        for n in range(CHUNKS):
             b, c = divmod(n, HALVES)
-            first = c * CHUNK
+            codes, scales = operand[1], operand[2]
+            following = new_operand() if n + 1 < CHUNKS else None
+            rows_stored = ROWS // 2 if n == 0 else ROWS
+            stage_qk = stage_pool.tile([P, 2 * HEADS, ROWS, HEAD_DIM], F32)
+            stage_v = stage_pool.tile([P, HEADS, ROWS, HEAD_DIM], F32)
 
             def multiply(bank, group, j):
                 nc.tensor.matmul_mx(
@@ -214,33 +238,15 @@ def tile_ttcodegenattention_pa_t_kernel(
                     stop=True,
                 )
 
-            def store(out, staged):
+            def store(out, staged, j0, j1):
                 nc.sync.dma_start(
-                    out=out[b, :, first : first + CHUNK, :].rearrange(
-                        "h (p j) d -> p h (j d)", j=ROWS
-                    ),
-                    in_=staged.rearrange("p h j d -> p h (j d)"),
+                    out=out[b, :, c * CHUNK : (c + 1) * CHUNK, :].rearrange(
+                        "h (p j) d -> p h j d", j=ROWS
+                    )[:, :, j0:j1, :],
+                    in_=staged[:, :, j0:j1, :],
                 )
 
-            stage_qk = stage_pool.tile([P, 2 * HEADS, ROWS, HEAD_DIM], F32)
-            stage_v = stage_pool.tile([P, HEADS, ROWS, HEAD_DIM], F32)
             for j in range(ROWS):
-                for a in (2 * j, 2 * j + 1):
-                    group, row = divmod(a, ROWS)
-                    bank = psum_copy.tile([P, GROUP], F32)
-                    multiply(bank, group, row)
-                    if group == VALUES:
-                        nc.scalar.copy(
-                            out=stage_v[:, :, row, :],
-                            in_=bank[:].rearrange("p (h d) -> p h d", h=HEADS),
-                        )
-                    else:
-                        nc.scalar.copy(
-                            out=stage_qk[:, :, row, ROTARY:],
-                            in_=bank[:].rearrange("p (g d) -> p g d", g=2 * HEADS),
-                        )
-                    if a == ROWS - 1:
-                        store(out_2, stage_v[:])
                 rope = psum_rope.tile([P, GROUP], F32)
                 multiply(rope, ROTATED, j)
                 full = [P, 2, 2 * HEADS, PAIRS, 2]
@@ -260,11 +266,35 @@ def tile_ttcodegenattention_pa_t_kernel(
                     in1=prod[:, 1].rearrange("p g i e -> p g (i e)"),
                     op=ALU.add,
                 )
-            store(out_0, stage_qk[:, 0:HEADS])
-            store(out_1, stage_qk[:, HEADS : 2 * HEADS])
-
-        quantised = quantise_chunk(0)
-        for n in range(CHUNKS):
-            following = quantise_chunk(n + 1) if n + 1 < CHUNKS else None
-            project_chunk(n, quantised[0], quantised[1])
-            quantised = following
+                for a in (2 * j, 2 * j + 1):
+                    group, row = divmod(a, ROWS)
+                    bank = psum_copy.tile([P, GROUP], F32)
+                    multiply(bank, group, row)
+                    if group == VALUES:
+                        nc.scalar.copy(
+                            out=stage_v[:, :, row, :],
+                            in_=bank[:].rearrange("p (h d) -> p h d", h=HEADS),
+                        )
+                    else:
+                        nc.scalar.copy(
+                            out=stage_qk[:, :, row, ROTARY:],
+                            in_=bank[:].rearrange("p (g d) -> p g d", g=2 * HEADS),
+                        )
+                    if (row + 1) % rows_stored == 0:
+                        j0, j1 = row + 1 - rows_stored, row + 1
+                        if group == VALUES:
+                            store(out_2, stage_v, j0, j1)
+                        else:
+                            store(out_0, stage_qk[:, 0:HEADS], j0, j1)
+                            store(out_1, stage_qk[:, HEADS : 2 * HEADS], j0, j1)
+                if n + 1 < CHUNKS:
+                    if j % 2 == 0:
+                        flip_rows(n + 1, j, following)
+                    if j % 4 == 3:
+                        quantise_rows(j - 3, j + 1, following)
+                if n + 1 < HALVES:
+                    if j == 0:
+                        squared = half_angle_squares(n + 1)
+                    if j == 2:
+                        fill_table(n + 1, squared)
+            operand = following

@@ -43,10 +43,9 @@ def tile_ttcodegenattention_pa_t_kernel(
         angle_pool = ctx.enter_context(tc.tile_pool(name="angles", bufs=2))
         x_pool = ctx.enter_context(tc.tile_pool(name="x", bufs=CHUNKS))
         quant_pool = ctx.enter_context(tc.tile_pool(name="quant", bufs=2))
-        prod_pool = ctx.enter_context(tc.tile_pool(name="prod", bufs=3))
+        prod_pool = ctx.enter_context(tc.tile_pool(name="prod", bufs=6))
         stage_pool = ctx.enter_context(tc.tile_pool(name="stage", bufs=2))
-        psum_x = ctx.enter_context(tc.psum_pool(name="psum_x", bufs=2))
-        psum_copy = ctx.enter_context(tc.psum_pool(name="psum_copy", bufs=3))
+        psum_copy = ctx.enter_context(tc.psum_pool(name="psum_copy", bufs=5))
         psum_rope = ctx.enter_context(tc.psum_pool(name="psum_rope", bufs=3))
         ctx.enter_context(tc.manual_schedule())
 
@@ -55,7 +54,7 @@ def tile_ttcodegenattention_pa_t_kernel(
             x_tiles.append(x_pool.tile([P, ROWS, EMBED], BF16, name="x_chunk"))
 
         def load_x(n, j0, j1):
-            b, c = divmod(n, HALVES)
+            c, b = divmod(n, BATCH)
             rows = hidden_states[b, c * CHUNK : (c + 1) * CHUNK, :]
             nc.sync.dma_start(
                 out=x_tiles[n][:, j0:j1, :],
@@ -176,7 +175,7 @@ def tile_ttcodegenattention_pa_t_kernel(
         def flip_rows(n, j, operand):
             x_words = x_tiles[n][:].bitcast(F32)
             grouped_words = operand[0][:].bitcast(F32)
-            flipped = psum_x.tile([P, 2, 2, P], F32)
+            flipped = psum_copy.tile([P, 2, 2, P], F32, tag="bank")
             for a in range(2):
                 for u in range(2):
                     nc.tensor.transpose(
@@ -217,23 +216,26 @@ def tile_ttcodegenattention_pa_t_kernel(
             )
 
         quantise_rows(0, ROWS // 2, operand)
-        quantise_rows(ROWS // 2, ROWS, operand)
+
+        outs = (out_0, out_1)
+        side = GROUP // 2
 
         for n in range(CHUNKS):
-            b, c = divmod(n, HALVES)
+            c, b = divmod(n, BATCH)
             codes, scales = operand[1], operand[2]
             following = new_operand() if n + 1 < CHUNKS else None
-            rows_stored = ROWS // 2 if n == 0 else ROWS
-            stage_qk = stage_pool.tile([P, 2 * HEADS, ROWS, HEAD_DIM], F32)
             stage_v = stage_pool.tile([P, HEADS, ROWS, HEAD_DIM], F32)
+            stage_q = stage_pool.tile([P, HEADS, ROWS, HEAD_DIM], F32)
+            stage_k = stage_pool.tile([P, HEADS, ROWS, HEAD_DIM], F32)
+            stages = (stage_q, stage_k)
 
-            def multiply(bank, group, j):
+            def multiply(out, group, first, width, j):
                 nc.tensor.matmul_mx(
-                    out=bank[:],
+                    out=out,
                     lhsT=codes[:, j, :].bitcast(FP8X4),
                     lhsT_scale=scales[:, j, :],
-                    rhs=w_words[:, group, :].bitcast(FP4X4),
-                    rhs_scale=w_planes[:, group, :],
+                    rhs=w_words[:, group, 2 * first : 2 * (first + width)].bitcast(FP4X4),
+                    rhs_scale=w_planes[:, group, first : first + width],
                     start=True,
                     stop=True,
                 )
@@ -246,55 +248,65 @@ def tile_ttcodegenattention_pa_t_kernel(
                     in_=staged[:, :, j0:j1, :],
                 )
 
-            for j in range(ROWS):
-                rope = psum_rope.tile([P, GROUP], F32)
-                multiply(rope, ROTATED, j)
-                full = [P, 2, 2 * HEADS, PAIRS, 2]
-                prod = prod_pool.tile(full, F32)
-                nc.vector.tensor_tensor(
-                    out=prod[:],
-                    in0=rope[:]
-                    .rearrange("p (g i m) -> p m g i", g=2 * HEADS, m=2)
-                    .unsqueeze(4)
-                    .to_broadcast(full),
-                    in1=table[:, :, c, j].unsqueeze(2).to_broadcast(full),
-                    op=ALU.mult,
-                )
+            for step in range(ROWS):
+                t, pair = divmod(step, ROWS // 2)
+                rope = psum_rope.tile([P, 2, side], F32)
+                prod = prod_pool.tile([P, 2, 2, HEADS, PAIRS, 2], F32)
+                full = [P, 2, HEADS, PAIRS, 2]
+                for a in range(2):
+                    multiply(rope[:, a, :], ROTATED, t * side, side, 2 * pair + a)
+                for a in range(2):
+                    nc.vector.tensor_tensor(
+                        out=prod[:, a],
+                        in0=rope[:, a, :]
+                        .rearrange("p (h i m) -> p m h i", h=HEADS, m=2)
+                        .unsqueeze(4)
+                        .to_broadcast(full),
+                        in1=table[:, :, c, 2 * pair + a].unsqueeze(2).to_broadcast(full),
+                        op=ALU.mult,
+                    )
                 nc.gpsimd.tensor_tensor(
-                    out=stage_qk[:, :, j, 0:ROTARY],
-                    in0=prod[:, 0].rearrange("p g i e -> p g (i e)"),
-                    in1=prod[:, 1].rearrange("p g i e -> p g (i e)"),
+                    out=stages[t][:, :, 2 * pair : 2 * pair + 2, 0:ROTARY].rearrange(
+                        "p h a d -> p a h d"
+                    ),
+                    in0=prod[:, :, 0].rearrange("p a h i e -> p a h (i e)"),
+                    in1=prod[:, :, 1].rearrange("p a h i e -> p a h (i e)"),
                     op=ALU.add,
                 )
-                for a in (2 * j, 2 * j + 1):
-                    group, row = divmod(a, ROWS)
-                    bank = psum_copy.tile([P, GROUP], F32)
-                    multiply(bank, group, row)
-                    if group == VALUES:
+                for unit in (2 * step, 2 * step + 1):
+                    bank = psum_copy.tile([P, 2, side], F32, tag="bank")
+                    if unit < ROWS:
+                        multiply(bank[:].rearrange("p a s -> p (a s)"), VALUES, 0, GROUP, unit)
                         nc.scalar.copy(
-                            out=stage_v[:, :, row, :],
-                            in_=bank[:].rearrange("p (h d) -> p h d", h=HEADS),
+                            out=stage_v[:, :, unit, :],
+                            in_=bank[:].rearrange("p a (h d) -> p (a h) d", d=HEAD_DIM),
                         )
+                        rows_stored = ROWS // 2 if n == 0 else ROWS
+                        if (unit + 1) % rows_stored == 0:
+                            store(out_2, stage_v, unit + 1 - rows_stored, unit + 1)
                     else:
+                        t_passed, pair_passed = divmod(unit - ROWS, ROWS // 2)
+                        j = 2 * pair_passed
+                        for a in range(2):
+                            multiply(bank[:, a, :], PASSED, t_passed * side, side, j + a)
                         nc.scalar.copy(
-                            out=stage_qk[:, :, row, ROTARY:],
-                            in_=bank[:].rearrange("p (g d) -> p g d", g=2 * HEADS),
+                            out=stages[t_passed][:, :, j : j + 2, ROTARY:].rearrange(
+                                "p h a d -> p a h d"
+                            ),
+                            in_=bank[:].rearrange("p a (h d) -> p a h d", h=HEADS),
                         )
-                    if (row + 1) % rows_stored == 0:
-                        j0, j1 = row + 1 - rows_stored, row + 1
-                        if group == VALUES:
-                            store(out_2, stage_v, j0, j1)
-                        else:
-                            store(out_0, stage_qk[:, 0:HEADS], j0, j1)
-                            store(out_1, stage_qk[:, HEADS : 2 * HEADS], j0, j1)
+                        if j + 2 == ROWS:
+                            store(outs[t_passed], stages[t_passed], 0, ROWS)
+                if step == 0:
+                    quantise_rows(ROWS // 2, ROWS, operand)
                 if n + 1 < CHUNKS:
-                    if j % 2 == 0:
-                        flip_rows(n + 1, j, following)
-                    if j % 4 == 3:
-                        quantise_rows(j - 3, j + 1, following)
-                if n + 1 < HALVES:
-                    if j == 0:
-                        squared = half_angle_squares(n + 1)
-                    if j == 2:
-                        fill_table(n + 1, squared)
+                    if step % 2 == 0:
+                        flip_rows(n + 1, step, following)
+                    if step == ROWS // 2:
+                        quantise_rows(0, ROWS // 2, following)
+                if b == BATCH - 1 and c + 1 < HALVES:
+                    if step == 0:
+                        squared = half_angle_squares(c + 1)
+                    if step == 2:
+                        fill_table(c + 1, squared)
             operand = following

@@ -47,7 +47,6 @@ def tile_ttcodegenattention_pa_t_kernel(
         stage_pool = ctx.enter_context(tc.tile_pool(name="stage", bufs=2))
         psum_copy = ctx.enter_context(tc.psum_pool(name="psum_copy", bufs=5))
         psum_rope = ctx.enter_context(tc.psum_pool(name="psum_rope", bufs=3))
-        ctx.enter_context(tc.manual_schedule())
 
         x_tiles = []
         for n in range(CHUNKS):

@@ -20,14 +20,11 @@ HEADS, HEAD_DIM, ROTARY = 4, 128, 64
 PAIRS = ROTARY // 2
 ROPE_BASE = 10000.0
 
-ROWS = 8
-CHUNK = P * ROWS
-HALVES = SEQ // CHUNK
-CHUNKS = BATCH * HALVES
-
-GROUP = 512
-VALUES, PASSED, ROTATED = 0, 1, 2
+ROWS = SEQ // P
+GROUP = 4
+GROUPS = ROWS // GROUP
 QUERY, VALUE, KEY = 0, 1, 2
+ROTATED, PASSED = 0, 1
 
 ROUND = 1.5 * 2.0**23
 
@@ -41,69 +38,49 @@ def tile_ttcodegenattention_pa_t_kernel(
     with ExitStack() as ctx:
         consts = ctx.enter_context(tc.tile_pool(name="consts", bufs=1))
         angle_pool = ctx.enter_context(tc.tile_pool(name="angles", bufs=2))
-        x_pool = ctx.enter_context(tc.tile_pool(name="x", bufs=CHUNKS))
-        quant_pool = ctx.enter_context(tc.tile_pool(name="quant", bufs=2))
-        prod_pool = ctx.enter_context(tc.tile_pool(name="prod", bufs=6))
-        stage_pool = ctx.enter_context(tc.tile_pool(name="stage", bufs=2))
-        psum_copy = ctx.enter_context(tc.psum_pool(name="psum_copy", bufs=5))
-        psum_rope = ctx.enter_context(tc.psum_pool(name="psum_rope", bufs=3))
+        x_pool = ctx.enter_context(tc.tile_pool(name="x", bufs=BATCH))
+        grouped_pool = ctx.enter_context(tc.tile_pool(name="grouped", bufs=2))
+        quant_pool = ctx.enter_context(tc.tile_pool(name="quant", bufs=BATCH))
+        prod_pool = ctx.enter_context(tc.tile_pool(name="prod", bufs=3))
+        stage_pool = ctx.enter_context(tc.tile_pool(name="stage", bufs=5))
+        psum_flip = ctx.enter_context(tc.psum_pool(name="psum_flip", bufs=2))
+        psum_mm = ctx.enter_context(tc.psum_pool(name="psum_mm", bufs=6))
+        ctx.enter_context(tc.manual_schedule())
 
         x_tiles = []
-        for n in range(CHUNKS):
-            x_tiles.append(x_pool.tile([P, ROWS, EMBED], BF16, name="x_chunk"))
+        for b in range(BATCH):
+            x_tiles.append(x_pool.tile([P, ROWS, EMBED], BF16, name="x_rows"))
 
-        def load_x(n, j0, j1):
-            c, b = divmod(n, BATCH)
-            rows = hidden_states[b, c * CHUNK : (c + 1) * CHUNK, :]
+        def load_x(b, j0, j1):
             nc.sync.dma_start(
-                out=x_tiles[n][:, j0:j1, :],
-                in_=rows.rearrange("(p j) k -> p j k", j=ROWS)[:, j0:j1, :],
+                out=x_tiles[b][:, j0:j1, :],
+                in_=hidden_states[b].rearrange("(p j) k -> p j k", j=ROWS)[:, j0:j1, :],
             )
 
-        load_x(0, 0, ROWS // 2)
-        load_x(0, ROWS // 2, ROWS)
+        load_x(0, 0, GROUP)
 
-        raw_planes = consts.tile([P, 3 * GROUP], U8, align_bytes=64)
-        nc.vector.memset(raw_planes[:].bitcast(I32), 0)
+        w_words = consts.tile([P, 2 * 3 * EMBED], U8, align_bytes=64)
+        nc.sync.dma_start(out=w_words[:].bitcast(I32), in_=w_qkv_words[0].bitcast(I32))
+        w_planes = consts.tile([P, 3 * EMBED], U8, align_bytes=64)
+        nc.vector.memset(w_planes[:].bitcast(I32), 0)
         scale_rows = w_qkv_scales[0].bitcast(I32)
         for quadrant in range(4):
             nc.sync.dma_start(
-                out=raw_planes[32 * quadrant : 32 * quadrant + 4, :].bitcast(I32),
+                out=w_planes[32 * quadrant : 32 * quadrant + 4, :].bitcast(I32),
                 in_=scale_rows[4 * quadrant : 4 * quadrant + 4, :],
             )
+        load_x(0, GROUP, 2 * GROUP)
+        load_x(0, 2 * GROUP, ROWS)
+        load_x(1, 0, ROWS)
 
-        w_words = consts.tile([P, 3, 2 * GROUP], U8, align_bytes=64)
-        words_sb = w_words[:].bitcast(I32)
-        words_in = w_qkv_words[0].bitcast(I32).rearrange("p (h t c) -> p h t c", h=HEADS, t=3)
-        half = HEAD_DIM // 4
-
-        def load_words(group, side, block, first):
-            width = words_sb.shape[2] // 2
-            nc.sync.dma_start(
-                out=words_sb[:, group, side * width : (side + 1) * width].rearrange(
-                    "p (h c) -> p h c", h=HEADS
-                ),
-                in_=words_in[:, :, block, first : first + half],
-            )
-
-        nc.sync.dma_start(
-            out=words_sb[:, VALUES, :].rearrange("p (h c) -> p h c", h=HEADS),
-            in_=words_in[:, :, VALUE, :],
-        )
-        load_words(ROTATED, 0, QUERY, 0)
-        load_words(ROTATED, 1, KEY, 0)
-        load_words(PASSED, 0, QUERY, half)
-        load_words(PASSED, 1, KEY, half)
-        for n in range(1, CHUNKS):
-            load_x(n, 0, ROWS)
-
-        position_int = consts.tile([P, HALVES, ROWS], I32)
-        nc.gpsimd.iota(
-            position_int[:], pattern=[[CHUNK, HALVES], [1, ROWS]], base=0, channel_multiplier=ROWS
-        )
+        warm = consts.tile([P, 2], F32)
+        nc.gpsimd.memset(warm[:], 0.0)
+        nc.scalar.activation(out=warm[:, 1:2], in_=warm[:, 0:1], func=FUNC.Sin)
+        position_int = consts.tile([P, ROWS], I32)
+        nc.gpsimd.iota(position_int[:], pattern=[[1, ROWS]], base=0, channel_multiplier=ROWS)
         ident = consts.tile([P, P], F32)
         make_identity(nc, ident[:])
-        position = consts.tile([P, HALVES, ROWS], F32)
+        position = consts.tile([P, ROWS], F32)
         nc.vector.tensor_copy(out=position[:], in_=position_int[:])
         ratio = ROPE_BASE ** (-1.0 / PAIRS)
         frequency = consts.tile([P, PAIRS], F32)
@@ -120,20 +97,21 @@ def tile_ttcodegenattention_pa_t_kernel(
             )
             filled *= 2
 
-        table = consts.tile([P, 2, HALVES, ROWS, PAIRS, 2], F32)
+        table = consts.tile([P, ROWS, 2, PAIRS, 2], F32)
+        HALF = ROWS // 2
 
         def half_angle_squares(c):
-            shape = [P, ROWS, PAIRS]
+            shape = [P, HALF, PAIRS]
             turns = angle_pool.tile(shape, F32)
             nc.vector.tensor_tensor(
                 out=turns[:],
-                in0=position[:, c, :].unsqueeze(2).to_broadcast(shape),
+                in0=position[:, c * HALF : (c + 1) * HALF].unsqueeze(2).to_broadcast(shape),
                 in1=frequency[:].unsqueeze(1).to_broadcast(shape),
                 op=ALU.mult,
             )
             whole = angle_pool.tile(shape, F32)
             nc.vector.tensor_scalar_add(out=whole[:], in0=turns[:], scalar1=ROUND)
-            part = angle_pool.tile([P, 2, ROWS, PAIRS], F32)
+            part = angle_pool.tile([P, 2, HALF, PAIRS], F32)
             nc.vector.scalar_tensor_tensor(
                 out=part[:, 0],
                 in0=whole[:],
@@ -143,9 +121,9 @@ def tile_ttcodegenattention_pa_t_kernel(
                 op1=ALU.subtract,
             )
             nc.vector.tensor_scalar_add(out=part[:, 1], in0=part[:, 0], scalar1=0.25)
-            half_sin = angle_pool.tile([P, 2, ROWS, PAIRS], F32)
+            half_sin = angle_pool.tile([P, 2, HALF, PAIRS], F32)
             nc.scalar.activation(out=half_sin[:], in_=part[:], func=FUNC.Sin, scale=math.pi)
-            squared = angle_pool.tile([P, 2, ROWS, PAIRS], F32)
+            squared = angle_pool.tile([P, 2, HALF, PAIRS], F32)
             nc.scalar.activation(out=squared[:], in_=half_sin[:], func=FUNC.Square)
             return squared
 
@@ -157,7 +135,7 @@ def tile_ttcodegenattention_pa_t_kernel(
                 (nc.gpsimd, 1, 1, 0, 1.0),
             ):
                 engine.tensor_scalar(
-                    out=table[:, m, c, :, :, e],
+                    out=table[:, c * HALF : (c + 1) * HALF, m, :, e],
                     in0=squared[:, phase],
                     scalar1=-2.0 * sign,
                     scalar2=sign,
@@ -165,147 +143,157 @@ def tile_ttcodegenattention_pa_t_kernel(
                     op1=ALU.add,
                 )
 
-        def new_operand():
-            grouped = quant_pool.tile([P, ROWS, P, 4], BF16, align_bytes=64)
-            codes = quant_pool.tile([P, ROWS, P], U32, align_bytes=64)
-            scales = quant_pool.tile([P, ROWS, P], U8, align_bytes=64)
-            return grouped, codes, scales
-
-        def flip_rows(n, j, operand):
-            x_words = x_tiles[n][:].bitcast(F32)
-            grouped_words = operand[0][:].bitcast(F32)
-            flipped = psum_copy.tile([P, 2, 2, P], F32, tag="bank")
-            for a in range(2):
-                for u in range(2):
-                    nc.tensor.transpose(
-                        flipped[:, a, u, :], x_words[:, j + a, u : EMBED // 2 : 2], ident[:]
-                    )
-            nc.scalar.copy(
-                out=grouped_words[:, j : j + 2], in_=flipped[:].rearrange("p a u r -> p a r u")
-            )
-
-        def quantise_rows(j0, j1, operand):
-            grouped, codes, scales = operand
-            nc.vector.quantize_mx(
-                out=codes[:, j0:j1].rearrange("p j r -> p (j r)").bitcast(FP8X4),
-                scales=scales[:, j0:j1].rearrange("p j r -> p (j r)"),
-                in_=grouped[:, j0:j1].rearrange("p j r t -> p (j r t)"),
-            )
-
         squared = half_angle_squares(0)
-        operand = new_operand()
-        for j in range(0, ROWS, 2):
-            flip_rows(0, j, operand)
         fill_table(0, squared)
 
-        w_planes = consts.tile([P, 3, GROUP], U8, align_bytes=64)
-        planes_sb = w_planes[:].bitcast(I32)
-        planes_in = raw_planes[:].bitcast(I32).rearrange("p (h t c) -> p h t c", h=HEADS, t=3)
-        quarter = HEAD_DIM // 8
-        nc.vector.tensor_copy(
-            out=planes_sb[:, VALUES, :].rearrange("p (h c) -> p h c", h=HEADS),
-            in_=planes_in[:, :, VALUE, :],
-        )
-        for group, first in ((ROTATED, 0), (PASSED, quarter)):
+        qk_words = consts.tile([P, HEADS, 2, 2 * HEAD_DIM], U8, align_bytes=64)
+        qk_planes = consts.tile([P, HEADS, 2, HEAD_DIM], U8, align_bytes=64)
+        words_in = w_words[:].rearrange("p (h t c) -> p h t c", h=HEADS, t=3)
+        planes_in = w_planes[:].rearrange("p (h t c) -> p h t c", h=HEADS, t=3)
+        for s, t in enumerate((QUERY, KEY)):
+            for m in range(2):
+                first = 2 * ROTARY * s + ROTARY * m
+                nc.vector.tensor_copy(
+                    out=qk_words[:, :, ROTATED, first : first + ROTARY].rearrange(
+                        "p h (i y) -> p h i y", y=2
+                    ),
+                    in_=words_in[:, :, t, 0 : 2 * ROTARY].rearrange(
+                        "p h (i m y) -> p h i m y", m=2, y=2
+                    )[:, :, :, m, :],
+                )
             nc.vector.tensor_copy(
-                out=planes_sb[:, group, :].rearrange("p (t h c) -> p t h c", t=2, h=HEADS),
-                in_=planes_in[:, :, QUERY : KEY + 1 : 2, first : first + quarter].rearrange(
-                    "p h t c -> p t h c"
+                out=qk_planes[:, :, ROTATED, ROTARY * s : ROTARY * (s + 1)].rearrange(
+                    "p h (m i) -> p h i m", m=2
                 ),
+                in_=planes_in[:, :, t, 0:ROTARY].rearrange("p h (i m) -> p h i m", m=2),
+            )
+        for regrouped, raw, width in ((qk_words, w_words, ROTARY // 2), (qk_planes, w_planes, ROTARY // 4)):
+            nc.vector.tensor_copy(
+                out=regrouped[:].bitcast(I32)[:, :, PASSED, :].rearrange("p h (s c) -> p h s c", s=2),
+                in_=raw[:].bitcast(I32).rearrange("p (h t c) -> p h t c", h=HEADS, t=3)[
+                    :, :, QUERY : KEY + 1 : 2, width : 2 * width
+                ],
             )
 
-        quantise_rows(0, ROWS // 2, operand)
+        codes, scales = [], []
+        for b in range(BATCH):
+            codes.append(quant_pool.tile([P, ROWS, P], U32, align_bytes=64, name="codes"))
+            scales.append(quant_pool.tile([P, ROWS, P], U8, align_bytes=64, name="scales"))
 
-        outs = (out_0, out_1)
-        side = GROUP // 2
+        def flip_rows(b, g, copies):
+            x_words = x_tiles[b][:].bitcast(F32)
+            grouped = grouped_pool.tile([P, GROUP, P, 4], BF16, align_bytes=64)
+            grouped_words = grouped[:].bitcast(F32)
+            banks = []
+            for a0 in range(0, GROUP, 2):
+                flipped = psum_flip.tile([P, 2, 2, P], F32)
+                for a in range(2):
+                    for u in range(2):
+                        nc.tensor.transpose(
+                            flipped[:, a, u, :],
+                            x_words[:, g * GROUP + a0 + a, u : EMBED // 2 : 2],
+                            ident[:],
+                        )
+                banks.append(flipped)
+            for a0, flipped, copy in zip(range(0, GROUP, 2), banks, copies):
+                copy(
+                    out=grouped_words[:, a0 : a0 + 2],
+                    in_=flipped[:].rearrange("p a u r -> p a r u"),
+                )
+            return grouped
 
-        for n in range(CHUNKS):
-            c, b = divmod(n, BATCH)
-            codes, scales = operand[1], operand[2]
-            following = new_operand() if n + 1 < CHUNKS else None
-            stage_v = stage_pool.tile([P, HEADS, ROWS, HEAD_DIM], F32)
-            stage_q = stage_pool.tile([P, HEADS, ROWS, HEAD_DIM], F32)
-            stage_k = stage_pool.tile([P, HEADS, ROWS, HEAD_DIM], F32)
-            stages = (stage_q, stage_k)
+        def quantise_rows(b, g, grouped):
+            rows = slice(g * GROUP, (g + 1) * GROUP)
+            nc.vector.quantize_mx(
+                out=codes[b][:, rows].rearrange("p j r -> p (j r)").bitcast(FP8X4),
+                scales=scales[b][:, rows].rearrange("p j r -> p (j r)"),
+                in_=grouped[:].rearrange("p j r t -> p (j r t)"),
+            )
 
-            def multiply(out, group, first, width, j):
+        def multiply(b, g, words, planes):
+            bank = psum_mm.tile([P, GROUP, HEAD_DIM], F32, tag="bank")
+            for a in range(GROUP):
                 nc.tensor.matmul_mx(
-                    out=out,
-                    lhsT=codes[:, j, :].bitcast(FP8X4),
-                    lhsT_scale=scales[:, j, :],
-                    rhs=w_words[:, group, 2 * first : 2 * (first + width)].bitcast(FP4X4),
-                    rhs_scale=w_planes[:, group, first : first + width],
+                    out=bank[:, a, :],
+                    lhsT=codes[b][:, g * GROUP + a, :].bitcast(FP8X4),
+                    lhsT_scale=scales[b][:, g * GROUP + a, :],
+                    rhs=words.bitcast(FP4X4),
+                    rhs_scale=planes,
                     start=True,
                     stop=True,
                 )
+            return bank
 
-            def store(out, staged, j0, j1):
-                nc.sync.dma_start(
-                    out=out[b, :, c * CHUNK : (c + 1) * CHUNK, :].rearrange(
-                        "h (p j) d -> p h j d", j=ROWS
-                    )[:, :, j0:j1, :],
-                    in_=staged[:, :, j0:j1, :],
-                )
+        scalar_only = (nc.scalar.copy, nc.scalar.copy)
+        full = [P, GROUP, 2, ROTARY, 2]
 
-            for step in range(ROWS):
-                t, pair = divmod(step, ROWS // 2)
-                rope = psum_rope.tile([P, 2, side], F32)
-                prod = prod_pool.tile([P, 2, 2, HEADS, PAIRS, 2], F32)
-                full = [P, 2, HEADS, PAIRS, 2]
-                for a in range(2):
-                    multiply(rope[:, a, :], ROTATED, t * side, side, 2 * pair + a)
-                for a in range(2):
+        segments = ((0, 0, 2), (0, 2, 2), (1, 0, 4))
+        prepare = {
+            (0, 1): (0, 2),
+            (0, 2): (0, 3),
+            (1, 0): (1, 0),
+            (1, 1): (1, 1),
+            (1, 2): (1, 2),
+            (1, 3): (1, 3),
+        }
+        for g in range(2):
+            grouped = flip_rows(0, g, scalar_only)
+            quantise_rows(0, g, grouped)
+        for number, (b, g_first, g_count) in enumerate(segments):
+            j_first = g_first * GROUP
+            j_count = g_count * GROUP
+            for h in range(HEADS):
+                staged_v = stage_pool.tile([P, j_count, HEAD_DIM], F32)
+                staged_qk = stage_pool.tile([P, 2, j_count, HEAD_DIM], F32)
+                block = 3 * h + VALUE
+                ahead = prepare.get((number, h))
+                for slot in range(g_count):
+                    g = g_first + slot
+                    rows = slice(slot * GROUP, (slot + 1) * GROUP)
+                    if ahead and slot == 0:
+                        grouped = flip_rows(ahead[0], ahead[1], scalar_only)
+                    bank = multiply(
+                        b,
+                        g,
+                        w_words[:, 2 * HEAD_DIM * block : 2 * HEAD_DIM * (block + 1)],
+                        w_planes[:, HEAD_DIM * block : HEAD_DIM * (block + 1)],
+                    )
+                    nc.scalar.copy(out=staged_v[:, rows, :], in_=bank[:])
+                    bank = multiply(b, g, qk_words[:, h, ROTATED, :], qk_planes[:, h, ROTATED, :])
+                    prod = prod_pool.tile(full, F32)
                     nc.vector.tensor_tensor(
-                        out=prod[:, a],
-                        in0=rope[:, a, :]
-                        .rearrange("p (h i m) -> p m h i", h=HEADS, m=2)
+                        out=prod[:],
+                        in0=bank[:]
+                        .rearrange("p a (s c) -> p a s c", s=2)
                         .unsqueeze(4)
                         .to_broadcast(full),
-                        in1=table[:, :, c, 2 * pair + a].unsqueeze(2).to_broadcast(full),
+                        in1=table[:, g * GROUP : (g + 1) * GROUP]
+                        .rearrange("p a m i e -> p a (m i) e")
+                        .unsqueeze(2)
+                        .to_broadcast(full),
                         op=ALU.mult,
                     )
-                nc.gpsimd.tensor_tensor(
-                    out=stages[t][:, :, 2 * pair : 2 * pair + 2, 0:ROTARY].rearrange(
-                        "p h a d -> p a h d"
-                    ),
-                    in0=prod[:, :, 0].rearrange("p a h i e -> p a h (i e)"),
-                    in1=prod[:, :, 1].rearrange("p a h i e -> p a h (i e)"),
-                    op=ALU.add,
-                )
-                for unit in (2 * step, 2 * step + 1):
-                    bank = psum_copy.tile([P, 2, side], F32, tag="bank")
-                    if unit < ROWS:
-                        multiply(bank[:].rearrange("p a s -> p (a s)"), VALUES, 0, GROUP, unit)
-                        nc.scalar.copy(
-                            out=stage_v[:, :, unit, :],
-                            in_=bank[:].rearrange("p a (h d) -> p (a h) d", d=HEAD_DIM),
-                        )
-                        rows_stored = ROWS // 2 if n == 0 else ROWS
-                        if (unit + 1) % rows_stored == 0:
-                            store(out_2, stage_v, unit + 1 - rows_stored, unit + 1)
-                    else:
-                        t_passed, pair_passed = divmod(unit - ROWS, ROWS // 2)
-                        j = 2 * pair_passed
-                        for a in range(2):
-                            multiply(bank[:, a, :], PASSED, t_passed * side, side, j + a)
-                        nc.scalar.copy(
-                            out=stages[t_passed][:, :, j : j + 2, ROTARY:].rearrange(
-                                "p h a d -> p a h d"
-                            ),
-                            in_=bank[:].rearrange("p a (h d) -> p a h d", h=HEADS),
-                        )
-                        if j + 2 == ROWS:
-                            store(outs[t_passed], stages[t_passed], 0, ROWS)
-                if step == 0:
-                    quantise_rows(ROWS // 2, ROWS, operand)
-                if n + 1 < CHUNKS:
-                    if step % 2 == 0:
-                        flip_rows(n + 1, step, following)
-                    if step == ROWS // 2:
-                        quantise_rows(0, ROWS // 2, following)
-                if b == BATCH - 1 and c + 1 < HALVES:
-                    if step == 0:
-                        squared = half_angle_squares(c + 1)
-                    if step == 2:
-                        fill_table(c + 1, squared)
-            operand = following
+                    nc.gpsimd.tensor_tensor(
+                        out=staged_qk[:, :, rows, 0:ROTARY].rearrange("p s a d -> p a s d"),
+                        in0=prod[:, :, :, 0:PAIRS, :].rearrange("p a s i e -> p a s (i e)"),
+                        in1=prod[:, :, :, PAIRS:, :].rearrange("p a s i e -> p a s (i e)"),
+                        op=ALU.add,
+                    )
+                    bank = multiply(b, g, qk_words[:, h, PASSED, :], qk_planes[:, h, PASSED, :])
+                    nc.scalar.copy(
+                        out=staged_qk[:, :, rows, ROTARY:].rearrange("p s a d -> p a s d"),
+                        in_=bank[:].rearrange("p a (s d) -> p a s d", s=2),
+                    )
+                    if ahead and slot == 1:
+                        quantise_rows(ahead[0], ahead[1], grouped)
+                    if number == 0 and slot == 1 and h == 0:
+                        squared = half_angle_squares(1)
+                    if number == 0 and slot == 1 and h == 1:
+                        fill_table(1, squared)
+                for out, staged in ((out_2, staged_v[:]), (out_0, staged_qk[:, 0]), (out_1, staged_qk[:, 1])):
+                    nc.sync.dma_start(
+                        out=out[b, h].rearrange("(p j) d -> p j d", j=ROWS)[
+                            :, j_first : j_first + j_count, :
+                        ],
+                        in_=staged,
+                    )

@@ -42,9 +42,10 @@ def tile_ttcodegenattention_pa_t_kernel(
         grouped_pool = ctx.enter_context(tc.tile_pool(name="grouped", bufs=2))
         quant_pool = ctx.enter_context(tc.tile_pool(name="quant", bufs=BATCH))
         prod_pool = ctx.enter_context(tc.tile_pool(name="prod", bufs=3))
-        stage_pool = ctx.enter_context(tc.tile_pool(name="stage", bufs=5))
-        psum_flip = ctx.enter_context(tc.psum_pool(name="psum_flip", bufs=2))
-        psum_mm = ctx.enter_context(tc.psum_pool(name="psum_mm", bufs=6))
+        stage_v_pool = ctx.enter_context(tc.tile_pool(name="stage_v", bufs=3))
+        stage_qk_pool = ctx.enter_context(tc.tile_pool(name="stage_qk", bufs=8))
+        psum_rot = ctx.enter_context(tc.psum_pool(name="psum_rot", bufs=2))
+        psum_copy = ctx.enter_context(tc.psum_pool(name="psum_copy", bufs=6))
         ctx.enter_context(tc.manual_schedule())
 
         x_tiles = []
@@ -71,23 +72,25 @@ def tile_ttcodegenattention_pa_t_kernel(
             )
         load_x(0, GROUP, 2 * GROUP)
         load_x(0, 2 * GROUP, ROWS)
-        load_x(1, 0, ROWS)
+        load_x(1, 0, 2 * GROUP)
+        load_x(1, 2 * GROUP, ROWS)
 
         warm = consts.tile([P, 2], F32)
         nc.gpsimd.memset(warm[:], 0.0)
         nc.scalar.activation(out=warm[:, 1:2], in_=warm[:, 0:1], func=FUNC.Sin)
-        position_int = consts.tile([P, ROWS], I32)
-        nc.gpsimd.iota(position_int[:], pattern=[[1, ROWS]], base=0, channel_multiplier=ROWS)
+        position = consts.tile([P, ROWS], F32)
+        nc.gpsimd.iota(
+            position[:],
+            pattern=[[1, ROWS]],
+            base=0,
+            channel_multiplier=ROWS,
+            allow_small_or_imprecise_dtypes=True,
+        )
         ident = consts.tile([P, P], F32)
         make_identity(nc, ident[:])
-        position = consts.tile([P, ROWS], F32)
-        nc.vector.tensor_copy(out=position[:], in_=position_int[:])
         ratio = ROPE_BASE ** (-1.0 / PAIRS)
         frequency = consts.tile([P, PAIRS], F32)
         nc.vector.memset(frequency[:, 0:1], 1.0)
-        nc.vector.tensor_scalar_mul(
-            out=frequency[:, 0:1], in0=frequency[:, 0:1], scalar1=1.0 / (2.0 * math.pi)
-        )
         filled = 1
         while filled < PAIRS:
             nc.vector.tensor_scalar_mul(
@@ -100,14 +103,16 @@ def tile_ttcodegenattention_pa_t_kernel(
         table = consts.tile([P, ROWS, 2, PAIRS, 2], F32)
         HALF = ROWS // 2
 
-        def half_angle_squares(c):
+        def turn_parts(c):
             shape = [P, HALF, PAIRS]
             turns = angle_pool.tile(shape, F32)
-            nc.vector.tensor_tensor(
+            nc.vector.scalar_tensor_tensor(
                 out=turns[:],
                 in0=position[:, c * HALF : (c + 1) * HALF].unsqueeze(2).to_broadcast(shape),
+                scalar=1.0 / (2.0 * math.pi),
                 in1=frequency[:].unsqueeze(1).to_broadcast(shape),
-                op=ALU.mult,
+                op0=ALU.mult,
+                op1=ALU.mult,
             )
             whole = angle_pool.tile(shape, F32)
             nc.vector.tensor_scalar_add(out=whole[:], in0=turns[:], scalar1=ROUND)
@@ -121,30 +126,34 @@ def tile_ttcodegenattention_pa_t_kernel(
                 op1=ALU.subtract,
             )
             nc.vector.tensor_scalar_add(out=part[:, 1], in0=part[:, 0], scalar1=0.25)
+            return part
+
+        def half_angle_squares(part):
             half_sin = angle_pool.tile([P, 2, HALF, PAIRS], F32)
             nc.scalar.activation(out=half_sin[:], in_=part[:], func=FUNC.Sin, scale=math.pi)
             squared = angle_pool.tile([P, 2, HALF, PAIRS], F32)
             nc.scalar.activation(out=squared[:], in_=half_sin[:], func=FUNC.Square)
             return squared
 
-        def fill_table(c, squared):
+        def fill_table(c, squared, sources):
             for engine, m, e, phase, sign in (
                 (nc.vector, 0, 0, 0, 1.0),
                 (nc.vector, 0, 1, 1, 1.0),
                 (nc.gpsimd, 1, 0, 1, -1.0),
                 (nc.gpsimd, 1, 1, 0, 1.0),
             ):
-                engine.tensor_scalar(
-                    out=table[:, c * HALF : (c + 1) * HALF, m, :, e],
-                    in0=squared[:, phase],
-                    scalar1=-2.0 * sign,
-                    scalar2=sign,
-                    op0=ALU.mult,
-                    op1=ALU.add,
-                )
+                if m in sources:
+                    engine.tensor_scalar(
+                        out=table[:, c * HALF : (c + 1) * HALF, m, :, e],
+                        in0=squared[:, phase],
+                        scalar1=-2.0 * sign,
+                        scalar2=sign,
+                        op0=ALU.mult,
+                        op1=ALU.add,
+                    )
 
-        squared = half_angle_squares(0)
-        fill_table(0, squared)
+        parts = [turn_parts(0), turn_parts(1)]
+        squared = [half_angle_squares(parts[0])]
 
         qk_words = consts.tile([P, HEADS, 2, 2 * HEAD_DIM], U8, align_bytes=64)
         qk_planes = consts.tile([P, HEADS, 2, HEAD_DIM], U8, align_bytes=64)
@@ -186,7 +195,7 @@ def tile_ttcodegenattention_pa_t_kernel(
             grouped_words = grouped[:].bitcast(F32)
             banks = []
             for a0 in range(0, GROUP, 2):
-                flipped = psum_flip.tile([P, 2, 2, P], F32)
+                flipped = psum_copy.tile([P, 2, 2, P], F32, tag="bank")
                 for a in range(2):
                     for u in range(2):
                         nc.tensor.transpose(
@@ -210,8 +219,8 @@ def tile_ttcodegenattention_pa_t_kernel(
                 in_=grouped[:].rearrange("p j r t -> p (j r t)"),
             )
 
-        def multiply(b, g, words, planes):
-            bank = psum_mm.tile([P, GROUP, HEAD_DIM], F32, tag="bank")
+        def multiply(pool, b, g, words, planes):
+            bank = pool.tile([P, GROUP, HEAD_DIM], F32, tag="bank")
             for a in range(GROUP):
                 nc.tensor.matmul_mx(
                     out=bank[:, a, :],
@@ -227,73 +236,84 @@ def tile_ttcodegenattention_pa_t_kernel(
         scalar_only = (nc.scalar.copy, nc.scalar.copy)
         full = [P, GROUP, 2, ROTARY, 2]
 
-        segments = ((0, 0, 2), (0, 2, 2), (1, 0, 4))
-        prepare = {
-            (0, 1): (0, 2),
-            (0, 2): (0, 3),
-            (1, 0): (1, 0),
-            (1, 1): (1, 1),
-            (1, 2): (1, 2),
-            (1, 3): (1, 3),
-        }
-        for g in range(2):
-            grouped = flip_rows(0, g, scalar_only)
-            quantise_rows(0, g, grouped)
-        for number, (b, g_first, g_count) in enumerate(segments):
+        SLOTS = 2 * HEADS
+        segments = ((0, 0), (0, 2), (1, 0), (1, 2))
+        fill_table(0, squared[0], (0, 1))
+        grouped = flip_rows(0, 0, scalar_only)
+        quantise_rows(0, 0, grouped)
+        squared.append(half_angle_squares(parts[1]))
+        fill_table(1, squared[1], (1,))
+        grouped = flip_rows(0, 1, scalar_only)
+        quantise_rows(0, 1, grouped)
+        fill_table(1, squared[1], (0,))
+        for number, (b, g_first) in enumerate(segments):
             j_first = g_first * GROUP
-            j_count = g_count * GROUP
-            for h in range(HEADS):
-                staged_v = stage_pool.tile([P, j_count, HEAD_DIM], F32)
-                staged_qk = stage_pool.tile([P, 2, j_count, HEAD_DIM], F32)
-                block = 3 * h + VALUE
-                ahead = prepare.get((number, h))
-                for slot in range(g_count):
-                    g = g_first + slot
-                    rows = slice(slot * GROUP, (slot + 1) * GROUP)
-                    if ahead and slot == 0:
-                        grouped = flip_rows(ahead[0], ahead[1], scalar_only)
+            staged_v = stage_v_pool.tile([P, HEADS, 2 * GROUP, HEAD_DIM], F32)
+            if number == 0:
+                value_banks = [(h, u) for u in range(2) for h in range(HEADS)]
+                banks_a_slot = 2
+            else:
+                value_banks = [(h, u) for h in range(HEADS) for u in range(2)]
+                banks_a_slot = 1
+            following = segments[number + 1] if number + 1 < len(segments) else None
+            for slot in range(SLOTS):
+                h, u = divmod(slot, 2)
+                g = g_first + u
+                rows = slice(u * GROUP, (u + 1) * GROUP)
+                if u == 0:
+                    staged_qk = stage_qk_pool.tile([P, 2, 2 * GROUP, HEAD_DIM], F32)
+                bank = multiply(psum_rot, b, g, qk_words[:, h, ROTATED, :], qk_planes[:, h, ROTATED, :])
+                prod = prod_pool.tile(full, F32)
+                nc.vector.tensor_tensor(
+                    out=prod[:],
+                    in0=bank[:].rearrange("p a (s c) -> p a s c", s=2).unsqueeze(4).to_broadcast(full),
+                    in1=table[:, g * GROUP : (g + 1) * GROUP]
+                    .rearrange("p a m i e -> p a (m i) e")
+                    .unsqueeze(2)
+                    .to_broadcast(full),
+                    op=ALU.mult,
+                )
+                nc.gpsimd.tensor_tensor(
+                    out=staged_qk[:, :, rows, 0:ROTARY].rearrange("p s a d -> p a s d"),
+                    in0=prod[:, :, :, 0:PAIRS, :].rearrange("p a s i e -> p a s (i e)"),
+                    in1=prod[:, :, :, PAIRS:, :].rearrange("p a s i e -> p a s (i e)"),
+                    op=ALU.add,
+                )
+                for h_v, u_v in value_banks[slot * banks_a_slot : (slot + 1) * banks_a_slot]:
+                    block = 3 * h_v + VALUE
                     bank = multiply(
+                        psum_copy,
                         b,
-                        g,
+                        g_first + u_v,
                         w_words[:, 2 * HEAD_DIM * block : 2 * HEAD_DIM * (block + 1)],
                         w_planes[:, HEAD_DIM * block : HEAD_DIM * (block + 1)],
                     )
-                    nc.scalar.copy(out=staged_v[:, rows, :], in_=bank[:])
-                    bank = multiply(b, g, qk_words[:, h, ROTATED, :], qk_planes[:, h, ROTATED, :])
-                    prod = prod_pool.tile(full, F32)
-                    nc.vector.tensor_tensor(
-                        out=prod[:],
-                        in0=bank[:]
-                        .rearrange("p a (s c) -> p a s c", s=2)
-                        .unsqueeze(4)
-                        .to_broadcast(full),
-                        in1=table[:, g * GROUP : (g + 1) * GROUP]
-                        .rearrange("p a m i e -> p a (m i) e")
-                        .unsqueeze(2)
-                        .to_broadcast(full),
-                        op=ALU.mult,
-                    )
-                    nc.gpsimd.tensor_tensor(
-                        out=staged_qk[:, :, rows, 0:ROTARY].rearrange("p s a d -> p a s d"),
-                        in0=prod[:, :, :, 0:PAIRS, :].rearrange("p a s i e -> p a s (i e)"),
-                        in1=prod[:, :, :, PAIRS:, :].rearrange("p a s i e -> p a s (i e)"),
-                        op=ALU.add,
-                    )
-                    bank = multiply(b, g, qk_words[:, h, PASSED, :], qk_planes[:, h, PASSED, :])
                     nc.scalar.copy(
-                        out=staged_qk[:, :, rows, ROTARY:].rearrange("p s a d -> p a s d"),
-                        in_=bank[:].rearrange("p a (s d) -> p a s d", s=2),
+                        out=staged_v[:, h_v, u_v * GROUP : (u_v + 1) * GROUP, :], in_=bank[:]
                     )
-                    if ahead and slot == 1:
-                        quantise_rows(ahead[0], ahead[1], grouped)
-                    if number == 0 and slot == 1 and h == 0:
-                        squared = half_angle_squares(1)
-                    if number == 0 and slot == 1 and h == 1:
-                        fill_table(1, squared)
-                for out, staged in ((out_2, staged_v[:]), (out_0, staged_qk[:, 0]), (out_1, staged_qk[:, 1])):
-                    nc.sync.dma_start(
-                        out=out[b, h].rearrange("(p j) d -> p j d", j=ROWS)[
-                            :, j_first : j_first + j_count, :
-                        ],
-                        in_=staged,
-                    )
+                    if h_v % 2 == 1 and (number == 0 or u_v == 1):
+                        j0 = u_v * GROUP if number == 0 else 0
+                        j1 = (u_v + 1) * GROUP
+                        nc.sync.dma_start(
+                            out=out_2[b, h_v - 1 : h_v + 1].rearrange("h (p j) d -> p h j d", j=ROWS)[
+                                :, :, j_first + j0 : j_first + j1, :
+                            ],
+                            in_=staged_v[:, h_v - 1 : h_v + 1, j0:j1, :],
+                        )
+                bank = multiply(psum_copy, b, g, qk_words[:, h, PASSED, :], qk_planes[:, h, PASSED, :])
+                nc.scalar.copy(
+                    out=staged_qk[:, :, rows, ROTARY:].rearrange("p s a d -> p a s d"),
+                    in_=bank[:].rearrange("p a (s d) -> p a s d", s=2),
+                )
+                if following and slot in (4, 6):
+                    grouped = flip_rows(following[0], following[1] + (slot - 4) // 2, scalar_only)
+                if following and slot in (5, 7):
+                    quantise_rows(following[0], following[1] + (slot - 4) // 2, grouped)
+                if u == 1:
+                    for out, s in ((out_0, 0), (out_1, 1)):
+                        nc.sync.dma_start(
+                            out=out[b, h].rearrange("(p j) d -> p j d", j=ROWS)[
+                                :, j_first : j_first + 2 * GROUP, :
+                            ],
+                            in_=staged_qk[:, s],
+                        )

@@ -71,8 +71,8 @@ def tile_ttcodegenattention_pa_t_kernel(
                 in_=scale_rows[4 * quadrant : 4 * quadrant + 4, :],
             )
         load_x(0, GROUP, 2 * GROUP)
-        load_x(0, 2 * GROUP, ROWS)
         load_x(1, 0, 2 * GROUP)
+        load_x(0, 2 * GROUP, ROWS)
         load_x(1, 2 * GROUP, ROWS)
 
         warm = consts.tile([P, 2], F32)
@@ -102,31 +102,38 @@ def tile_ttcodegenattention_pa_t_kernel(
 
         table = consts.tile([P, ROWS, 2, PAIRS, 2], F32)
         HALF = ROWS // 2
+        shape = [P, HALF, PAIRS]
 
-        def turn_parts(c):
-            shape = [P, HALF, PAIRS]
+        def angle_tiles():
             turns = angle_pool.tile(shape, F32)
-            nc.vector.scalar_tensor_tensor(
-                out=turns[:],
-                in0=position[:, c * HALF : (c + 1) * HALF].unsqueeze(2).to_broadcast(shape),
-                scalar=1.0 / (2.0 * math.pi),
-                in1=frequency[:].unsqueeze(1).to_broadcast(shape),
-                op0=ALU.mult,
-                op1=ALU.mult,
-            )
             whole = angle_pool.tile(shape, F32)
-            nc.vector.tensor_scalar_add(out=whole[:], in0=turns[:], scalar1=ROUND)
             part = angle_pool.tile([P, 2, HALF, PAIRS], F32)
-            nc.vector.scalar_tensor_tensor(
-                out=part[:, 0],
-                in0=whole[:],
-                scalar=ROUND,
-                in1=turns[:],
-                op0=ALU.subtract,
-                op1=ALU.subtract,
-            )
-            nc.vector.tensor_scalar_add(out=part[:, 1], in0=part[:, 0], scalar1=0.25)
-            return part
+            return turns, whole, part
+
+        def angle_step(c, step, tiles):
+            turns, whole, part = tiles
+            if step == 0:
+                nc.vector.scalar_tensor_tensor(
+                    out=turns[:],
+                    in0=position[:, c * HALF : (c + 1) * HALF].unsqueeze(2).to_broadcast(shape),
+                    scalar=1.0 / (2.0 * math.pi),
+                    in1=frequency[:].unsqueeze(1).to_broadcast(shape),
+                    op0=ALU.mult,
+                    op1=ALU.mult,
+                )
+            elif step == 1:
+                nc.vector.tensor_scalar_add(out=whole[:], in0=turns[:], scalar1=ROUND)
+            elif step == 2:
+                nc.vector.scalar_tensor_tensor(
+                    out=part[:, 0],
+                    in0=whole[:],
+                    scalar=ROUND,
+                    in1=turns[:],
+                    op0=ALU.subtract,
+                    op1=ALU.subtract,
+                )
+            else:
+                nc.vector.tensor_scalar_add(out=part[:, 1], in0=part[:, 0], scalar1=0.25)
 
         def half_angle_squares(part):
             half_sin = angle_pool.tile([P, 2, HALF, PAIRS], F32)
@@ -135,64 +142,61 @@ def tile_ttcodegenattention_pa_t_kernel(
             nc.scalar.activation(out=squared[:], in_=half_sin[:], func=FUNC.Square)
             return squared
 
-        def fill_table(c, squared, sources):
-            for engine, m, e, phase, sign in (
-                (nc.vector, 0, 0, 0, 1.0),
-                (nc.vector, 0, 1, 1, 1.0),
-                (nc.gpsimd, 1, 0, 1, -1.0),
-                (nc.gpsimd, 1, 1, 0, 1.0),
-            ):
-                if m in sources:
-                    engine.tensor_scalar(
-                        out=table[:, c * HALF : (c + 1) * HALF, m, :, e],
-                        in0=squared[:, phase],
-                        scalar1=-2.0 * sign,
-                        scalar2=sign,
-                        op0=ALU.mult,
-                        op1=ALU.add,
-                    )
-
-        parts = [turn_parts(0), turn_parts(1)]
-        squared = [half_angle_squares(parts[0])]
+        def fill_table(engine, g, squared):
+            first = (g % 2) * GROUP
+            for m, e, phase, sign in ((0, 0, 0, 1.0), (0, 1, 1, 1.0), (1, 0, 1, -1.0), (1, 1, 0, 1.0)):
+                engine.tensor_scalar(
+                    out=table[:, g * GROUP : (g + 1) * GROUP, m, :, e],
+                    in0=squared[:, phase, first : first + GROUP, :],
+                    scalar1=-2.0 * sign,
+                    scalar2=sign,
+                    op0=ALU.mult,
+                    op1=ALU.add,
+                )
 
         qk_words = consts.tile([P, HEADS, 2, 2 * HEAD_DIM], U8, align_bytes=64)
         qk_planes = consts.tile([P, HEADS, 2, HEAD_DIM], U8, align_bytes=64)
-        words_in = w_words[:].rearrange("p (h t c) -> p h t c", h=HEADS, t=3)
-        planes_in = w_planes[:].rearrange("p (h t c) -> p h t c", h=HEADS, t=3)
-        for s, t in enumerate((QUERY, KEY)):
-            for m in range(2):
-                first = 2 * ROTARY * s + ROTARY * m
+
+        def regroup():
+            words_in = w_words[:].rearrange("p (h t c) -> p h t c", h=HEADS, t=3)
+            planes_in = w_planes[:].rearrange("p (h t c) -> p h t c", h=HEADS, t=3)
+            for s, t in enumerate((QUERY, KEY)):
+                for m in range(2):
+                    first = 2 * ROTARY * s + ROTARY * m
+                    nc.vector.tensor_copy(
+                        out=qk_words[:, :, ROTATED, first : first + ROTARY].rearrange(
+                            "p h (i y) -> p h i y", y=2
+                        ),
+                        in_=words_in[:, :, t, 0 : 2 * ROTARY].rearrange(
+                            "p h (i m y) -> p h i m y", m=2, y=2
+                        )[:, :, :, m, :],
+                    )
                 nc.vector.tensor_copy(
-                    out=qk_words[:, :, ROTATED, first : first + ROTARY].rearrange(
-                        "p h (i y) -> p h i y", y=2
+                    out=qk_planes[:, :, ROTATED, ROTARY * s : ROTARY * (s + 1)].rearrange(
+                        "p h (m i) -> p h i m", m=2
                     ),
-                    in_=words_in[:, :, t, 0 : 2 * ROTARY].rearrange(
-                        "p h (i m y) -> p h i m y", m=2, y=2
-                    )[:, :, :, m, :],
+                    in_=planes_in[:, :, t, 0:ROTARY].rearrange("p h (i m) -> p h i m", m=2),
                 )
-            nc.vector.tensor_copy(
-                out=qk_planes[:, :, ROTATED, ROTARY * s : ROTARY * (s + 1)].rearrange(
-                    "p h (m i) -> p h i m", m=2
-                ),
-                in_=planes_in[:, :, t, 0:ROTARY].rearrange("p h (i m) -> p h i m", m=2),
-            )
-        for regrouped, raw, width in ((qk_words, w_words, ROTARY // 2), (qk_planes, w_planes, ROTARY // 4)):
-            nc.vector.tensor_copy(
-                out=regrouped[:].bitcast(I32)[:, :, PASSED, :].rearrange("p h (s c) -> p h s c", s=2),
-                in_=raw[:].bitcast(I32).rearrange("p (h t c) -> p h t c", h=HEADS, t=3)[
-                    :, :, QUERY : KEY + 1 : 2, width : 2 * width
-                ],
-            )
+            for regrouped, raw, width in (
+                (qk_words, w_words, ROTARY // 2),
+                (qk_planes, w_planes, ROTARY // 4),
+            ):
+                nc.vector.tensor_copy(
+                    out=regrouped[:].bitcast(I32)[:, :, PASSED, :].rearrange(
+                        "p h (s c) -> p h s c", s=2
+                    ),
+                    in_=raw[:].bitcast(I32).rearrange("p (h t c) -> p h t c", h=HEADS, t=3)[
+                        :, :, QUERY : KEY + 1 : 2, width : 2 * width
+                    ],
+                )
 
         codes, scales = [], []
         for b in range(BATCH):
             codes.append(quant_pool.tile([P, ROWS, P], U32, align_bytes=64, name="codes"))
             scales.append(quant_pool.tile([P, ROWS, P], U8, align_bytes=64, name="scales"))
 
-        def flip_rows(b, g, copies):
+        def flip_rows(b, g):
             x_words = x_tiles[b][:].bitcast(F32)
-            grouped = grouped_pool.tile([P, GROUP, P, 4], BF16, align_bytes=64)
-            grouped_words = grouped[:].bitcast(F32)
             banks = []
             for a0 in range(0, GROUP, 2):
                 flipped = psum_copy.tile([P, 2, 2, P], F32, tag="bank")
@@ -204,8 +208,13 @@ def tile_ttcodegenattention_pa_t_kernel(
                             ident[:],
                         )
                 banks.append(flipped)
-            for a0, flipped, copy in zip(range(0, GROUP, 2), banks, copies):
-                copy(
+            return banks
+
+        def copy_flipped(banks):
+            grouped = grouped_pool.tile([P, GROUP, P, 4], BF16, align_bytes=64)
+            grouped_words = grouped[:].bitcast(F32)
+            for a0, flipped in zip(range(0, GROUP, 2), banks):
+                nc.scalar.copy(
                     out=grouped_words[:, a0 : a0 + 2],
                     in_=flipped[:].rearrange("p a u r -> p a r u"),
                 )
@@ -233,35 +242,76 @@ def tile_ttcodegenattention_pa_t_kernel(
                 )
             return bank
 
-        scalar_only = (nc.scalar.copy, nc.scalar.copy)
-        full = [P, GROUP, 2, ROTARY, 2]
+        def copy_values(b, g, h, staged):
+            block = 3 * h + VALUE
+            bank = multiply(
+                psum_copy,
+                b,
+                g,
+                w_words[:, 2 * HEAD_DIM * block : 2 * HEAD_DIM * (block + 1)],
+                w_planes[:, HEAD_DIM * block : HEAD_DIM * (block + 1)],
+            )
+            nc.scalar.copy(out=staged, in_=bank[:])
+
+        def copy_passed(b, g, h, staged):
+            bank = multiply(psum_copy, b, g, qk_words[:, h, PASSED, :], qk_planes[:, h, PASSED, :])
+            nc.scalar.copy(
+                out=staged.rearrange("p s a d -> p a s d"),
+                in_=bank[:].rearrange("p a (s d) -> p a s d", s=2),
+            )
+
+        tiles = angle_tiles()
+        for step in range(4):
+            angle_step(0, step, tiles)
+        banks_0 = flip_rows(0, 0)
+        banks_1 = flip_rows(0, 1)
+        grouped_0 = copy_flipped(banks_0)
+        squared = half_angle_squares(tiles[2])
+        grouped_1 = copy_flipped(banks_1)
+        fill_table(nc.gpsimd, 1, squared)
+        regroup()
+        quantise_rows(0, 0, grouped_0)
+        fill_table(nc.vector, 0, squared)
+        quantise_rows(0, 1, grouped_1)
 
         SLOTS = 2 * HEADS
-        segments = ((0, 0), (0, 2), (1, 0), (1, 2))
-        fill_table(0, squared[0], (0, 1))
-        grouped = flip_rows(0, 0, scalar_only)
-        quantise_rows(0, 0, grouped)
-        squared.append(half_angle_squares(parts[1]))
-        fill_table(1, squared[1], (1,))
-        grouped = flip_rows(0, 1, scalar_only)
-        quantise_rows(0, 1, grouped)
-        fill_table(1, squared[1], (0,))
+        segments = ((0, 0), (1, 0), (0, 2), (1, 2))
+        full = [P, GROUP, 2, ROTARY, 2]
         for number, (b, g_first) in enumerate(segments):
             j_first = g_first * GROUP
             staged_v = stage_v_pool.tile([P, HEADS, 2 * GROUP, HEAD_DIM], F32)
-            if number == 0:
-                value_banks = [(h, u) for u in range(2) for h in range(HEADS)]
-                banks_a_slot = 2
-            else:
-                value_banks = [(h, u) for h in range(HEADS) for u in range(2)]
-                banks_a_slot = 1
+            staged_heads = {}
             following = segments[number + 1] if number + 1 < len(segments) else None
+
+            def store_values(h0, j0, j1):
+                nc.sync.dma_start(
+                    out=out_2[b, h0 : h0 + 2].rearrange("h (p j) d -> p h j d", j=ROWS)[
+                        :, :, j_first + j0 : j_first + j1, :
+                    ],
+                    in_=staged_v[:, h0 : h0 + 2, j0:j1, :],
+                )
+
+            def passed_and_store(slot):
+                h, u = divmod(slot, 2)
+                staged = staged_heads[h]
+                copy_passed(b, g_first + u, h, staged[:, :, u * GROUP : (u + 1) * GROUP, ROTARY:])
+                if u == 1:
+                    for out, s in ((out_0, 0), (out_1, 1)):
+                        nc.sync.dma_start(
+                            out=out[b, h].rearrange("(p j) d -> p j d", j=ROWS)[
+                                :, j_first : j_first + 2 * GROUP, :
+                            ],
+                            in_=staged[:, s],
+                        )
+
             for slot in range(SLOTS):
                 h, u = divmod(slot, 2)
                 g = g_first + u
                 rows = slice(u * GROUP, (u + 1) * GROUP)
                 if u == 0:
-                    staged_qk = stage_qk_pool.tile([P, 2, 2 * GROUP, HEAD_DIM], F32)
+                    staged_heads[h] = stage_qk_pool.tile(
+                        [P, 2, 2 * GROUP, HEAD_DIM], F32, name="staged_qk"
+                    )
                 bank = multiply(psum_rot, b, g, qk_words[:, h, ROTATED, :], qk_planes[:, h, ROTATED, :])
                 prod = prod_pool.tile(full, F32)
                 nc.vector.tensor_tensor(
@@ -274,46 +324,45 @@ def tile_ttcodegenattention_pa_t_kernel(
                     op=ALU.mult,
                 )
                 nc.gpsimd.tensor_tensor(
-                    out=staged_qk[:, :, rows, 0:ROTARY].rearrange("p s a d -> p a s d"),
+                    out=staged_heads[h][:, :, rows, 0:ROTARY].rearrange("p s a d -> p a s d"),
                     in0=prod[:, :, :, 0:PAIRS, :].rearrange("p a s i e -> p a s (i e)"),
                     in1=prod[:, :, :, PAIRS:, :].rearrange("p a s i e -> p a s (i e)"),
                     op=ALU.add,
                 )
-                for h_v, u_v in value_banks[slot * banks_a_slot : (slot + 1) * banks_a_slot]:
-                    block = 3 * h_v + VALUE
-                    bank = multiply(
-                        psum_copy,
-                        b,
-                        g_first + u_v,
-                        w_words[:, 2 * HEAD_DIM * block : 2 * HEAD_DIM * (block + 1)],
-                        w_planes[:, HEAD_DIM * block : HEAD_DIM * (block + 1)],
-                    )
-                    nc.scalar.copy(
-                        out=staged_v[:, h_v, u_v * GROUP : (u_v + 1) * GROUP, :], in_=bank[:]
-                    )
-                    if h_v % 2 == 1 and (number == 0 or u_v == 1):
-                        j0 = u_v * GROUP if number == 0 else 0
-                        j1 = (u_v + 1) * GROUP
-                        nc.sync.dma_start(
-                            out=out_2[b, h_v - 1 : h_v + 1].rearrange("h (p j) d -> p h j d", j=ROWS)[
-                                :, :, j_first + j0 : j_first + j1, :
-                            ],
-                            in_=staged_v[:, h_v - 1 : h_v + 1, j0:j1, :],
-                        )
-                bank = multiply(psum_copy, b, g, qk_words[:, h, PASSED, :], qk_planes[:, h, PASSED, :])
-                nc.scalar.copy(
-                    out=staged_qk[:, :, rows, ROTARY:].rearrange("p s a d -> p a s d"),
-                    in_=bank[:].rearrange("p a (s d) -> p a s d", s=2),
-                )
-                if following and slot in (4, 6):
-                    grouped = flip_rows(following[0], following[1] + (slot - 4) // 2, scalar_only)
-                if following and slot in (5, 7):
-                    quantise_rows(following[0], following[1] + (slot - 4) // 2, grouped)
-                if u == 1:
-                    for out, s in ((out_0, 0), (out_1, 1)):
-                        nc.sync.dma_start(
-                            out=out[b, h].rearrange("(p j) d -> p j d", j=ROWS)[
-                                :, j_first : j_first + 2 * GROUP, :
-                            ],
-                            in_=staged_qk[:, s],
-                        )
+                if number == 0:
+                    if slot < 2:
+                        for h_v in range(HEADS):
+                            copy_values(b, g_first + slot, h_v, staged_v[:, h_v, rows, :])
+                            if h_v % 2 == 1:
+                                store_values(h_v - 1, slot * GROUP, (slot + 1) * GROUP)
+                    else:
+                        for earlier in range(2 if slot == 2 else 0):
+                            passed_and_store(earlier)
+                        passed_and_store(slot)
+                else:
+                    if slot < HEADS:
+                        for u_v in range(2):
+                            copy_values(
+                                b, g_first + u_v, slot, staged_v[:, slot, u_v * GROUP : (u_v + 1) * GROUP, :]
+                            )
+                        if slot % 2 == 1:
+                            store_values(slot - 1, 0, 2 * GROUP)
+                    passed_and_store(slot)
+                if following and slot in (5, 6):
+                    flipped_next = copy_flipped(flip_rows(following[0], following[1] + slot - 5))
+                    if slot == 6:
+                        quantise_rows(following[0], following[1], waiting)
+                    waiting = flipped_next
+                if following and slot == 7:
+                    quantise_rows(following[0], following[1] + 1, waiting)
+                if number == 1:
+                    if slot == 0:
+                        tiles = angle_tiles()
+                    if slot < 4:
+                        angle_step(1, slot, tiles)
+                    if slot == 4:
+                        squared = half_angle_squares(tiles[2])
+                    if slot == 5:
+                        fill_table(nc.vector, 2, squared)
+                    if slot == 7:
+                        fill_table(nc.vector, 3, squared)

@@ -21,6 +21,7 @@ PAIRS = ROTARY // 2
 ROPE_BASE = 10000.0
 
 ROWS = SEQ // P
+RUN = ROWS // 2
 GROUP = 4
 GROUPS = ROWS // GROUP
 QUERY, VALUE, KEY = 0, 1, 2
@@ -55,7 +56,9 @@ def tile_ttcodegenattention_pa_t_kernel(
         def load_x(b, j0, j1):
             nc.sync.dma_start(
                 out=x_tiles[b][:, j0:j1, :],
-                in_=hidden_states[b].rearrange("(p j) k -> p j k", j=ROWS)[:, j0:j1, :],
+                in_=hidden_states[b].rearrange("(c p r) k -> p c r k", c=2, r=RUN)[
+                    :, j0 // RUN, j0 % RUN : j0 % RUN + j1 - j0, :
+                ],
             )
 
         load_x(0, 0, GROUP)
@@ -81,9 +84,9 @@ def tile_ttcodegenattention_pa_t_kernel(
         position = consts.tile([P, ROWS], F32)
         nc.gpsimd.iota(
             position[:],
-            pattern=[[1, ROWS]],
+            pattern=[[SEQ // 2, 2], [1, RUN]],
             base=0,
-            channel_multiplier=ROWS,
+            channel_multiplier=RUN,
             allow_small_or_imprecise_dtypes=True,
         )
         ident = consts.tile([P, P], F32)
@@ -285,8 +288,8 @@ def tile_ttcodegenattention_pa_t_kernel(
 
             def store_values(h0, j0, j1):
                 nc.sync.dma_start(
-                    out=out_2[b, h0 : h0 + 2].rearrange("h (p j) d -> p h j d", j=ROWS)[
-                        :, :, j_first + j0 : j_first + j1, :
+                    out=out_2[b, h0 : h0 + 2].rearrange("h (c p r) d -> p h c r d", c=2, r=RUN)[
+                        :, :, j_first // RUN, j0:j1, :
                     ],
                     in_=staged_v[:, h0 : h0 + 2, j0:j1, :],
                 )
@@ -298,8 +301,8 @@ def tile_ttcodegenattention_pa_t_kernel(
                 if u == 1:
                     for out, s in ((out_0, 0), (out_1, 1)):
                         nc.sync.dma_start(
-                            out=out[b, h].rearrange("(p j) d -> p j d", j=ROWS)[
-                                :, j_first : j_first + 2 * GROUP, :
+                            out=out[b, h].rearrange("(c p r) d -> p c r d", c=2, r=RUN)[
+                                :, j_first // RUN, :, :
                             ],
                             in_=staged[:, s],
                         )

@@ -49,6 +49,9 @@ def tile_ttcodegenattention_pa_t_kernel(
         psum_copy = ctx.enter_context(tc.psum_pool(name="psum_copy", bufs=6))
         ctx.enter_context(tc.manual_schedule())
 
+        zeros = consts.tile([P, 4 * P], BF16)
+        nc.gpsimd.memset(zeros[:], 0.0)
+
         x_tiles = []
         for b in range(BATCH):
             x_tiles.append(x_pool.tile([P, ROWS, EMBED], BF16, name="x_rows"))
@@ -263,11 +266,22 @@ def tile_ttcodegenattention_pa_t_kernel(
                 in_=bank[:].rearrange("p a (s d) -> p a s d", s=2),
             )
 
+        idle_bank = psum_copy.tile([P, 4 * P], F32, tag="bank")
+
+        def keep_busy(count):
+            for n in range(count):
+                nc.tensor.matmul(
+                    idle_bank[:], lhsT=zeros[:, 0:P], rhs=zeros[:], start=True, stop=True
+                )
+
         tiles = angle_tiles()
         for step in range(4):
             angle_step(0, step, tiles)
+        keep_busy(5)
         banks_0 = flip_rows(0, 0)
+        keep_busy(2)
         banks_1 = flip_rows(0, 1)
+        keep_busy(3)
         grouped_0 = copy_flipped(banks_0)
         squared = half_angle_squares(tiles[2])
         grouped_1 = copy_flipped(banks_1)

@@ -113,11 +113,11 @@ def tile_ttcodegenattention_pa_t_kernel(
         def angle_tiles():
             turns = angle_pool.tile(shape, F32)
             whole = angle_pool.tile(shape, F32)
-            part = angle_pool.tile([P, 2, HALF, PAIRS], F32)
-            return turns, whole, part
+            parts = angle_pool.tile([P, 3, HALF, PAIRS], F32)
+            return turns, whole, parts
 
         def angle_step(c, step, tiles):
-            turns, whole, part = tiles
+            turns, whole, parts = tiles
             if step == 0:
                 nc.vector.scalar_tensor_tensor(
                     out=turns[:],
@@ -131,33 +131,27 @@ def tile_ttcodegenattention_pa_t_kernel(
                 nc.vector.tensor_scalar_add(out=whole[:], in0=turns[:], scalar1=ROUND)
             elif step == 2:
                 nc.vector.scalar_tensor_tensor(
-                    out=part[:, 0],
+                    out=parts[:, 0],
                     in0=whole[:],
                     scalar=ROUND,
                     in1=turns[:],
                     op0=ALU.subtract,
                     op1=ALU.subtract,
                 )
+            elif step == 3:
+                nc.vector.tensor_scalar_mul(out=parts[:, 2], in0=parts[:, 0], scalar1=-1.0)
+            elif step == 4:
+                nc.vector.tensor_tensor(out=parts[:, 1], in0=parts[:, 0], in1=parts[:, 2], op=ALU.min)
             else:
-                nc.vector.tensor_scalar_add(out=part[:, 1], in0=part[:, 0], scalar1=0.25)
+                nc.vector.tensor_scalar_add(out=parts[:, 1], in0=parts[:, 1], scalar1=0.25)
 
-        def half_angle_squares(part):
-            half_sin = angle_pool.tile([P, 2, HALF, PAIRS], F32)
-            nc.scalar.activation(out=half_sin[:], in_=part[:], func=FUNC.Sin, scale=math.pi)
-            squared = angle_pool.tile([P, 2, HALF, PAIRS], F32)
-            nc.scalar.activation(out=squared[:], in_=half_sin[:], func=FUNC.Square)
-            return squared
-
-        def fill_table(engine, g, squared):
-            first = (g % 2) * GROUP
-            for m, e, phase, sign in ((0, 0, 0, 1.0), (0, 1, 1, 1.0), (1, 0, 1, -1.0), (1, 1, 0, 1.0)):
-                engine.tensor_scalar(
-                    out=table[:, g * GROUP : (g + 1) * GROUP, m, :, e],
-                    in0=squared[:, phase, first : first + GROUP, :],
-                    scalar1=-2.0 * sign,
-                    scalar2=sign,
-                    op0=ALU.mult,
-                    op1=ALU.add,
+        def fill_table(c, parts):
+            for m in range(2):
+                nc.scalar.activation(
+                    out=table[:, c * HALF : (c + 1) * HALF, m],
+                    in_=parts[:, 1 - m : 3 - m].rearrange("p e r i -> p r i e"),
+                    func=FUNC.Sin,
+                    scale=2.0 * math.pi,
                 )
 
         qk_words = consts.tile([P, HEADS, 2, 2 * HEAD_DIM], U8, align_bytes=64)
@@ -179,9 +173,9 @@ def tile_ttcodegenattention_pa_t_kernel(
                     )
                 nc.vector.tensor_copy(
                     out=qk_planes[:, :, ROTATED, ROTARY * s : ROTARY * (s + 1)].rearrange(
-                        "p h (m i) -> p h i m", m=2
+                        "p h (m i) -> p h m i", m=2
                     ),
-                    in_=planes_in[:, :, t, 0:ROTARY].rearrange("p h (i m) -> p h i m", m=2),
+                    in_=planes_in[:, :, t, 0:ROTARY].rearrange("p h (i m) -> p h m i", m=2),
                 )
             for regrouped, raw, width in (
                 (qk_words, w_words, ROTARY // 2),
@@ -275,7 +269,7 @@ def tile_ttcodegenattention_pa_t_kernel(
                 )
 
         tiles = angle_tiles()
-        for step in range(4):
+        for step in range(6):
             angle_step(0, step, tiles)
         keep_busy(5)
         banks_0 = flip_rows(0, 0)
@@ -283,12 +277,10 @@ def tile_ttcodegenattention_pa_t_kernel(
         banks_1 = flip_rows(0, 1)
         keep_busy(3)
         grouped_0 = copy_flipped(banks_0)
-        squared = half_angle_squares(tiles[2])
+        fill_table(0, tiles[2])
         grouped_1 = copy_flipped(banks_1)
-        fill_table(nc.gpsimd, 1, squared)
         regroup()
         quantise_rows(0, 0, grouped_0)
-        fill_table(nc.vector, 0, squared)
         quantise_rows(0, 1, grouped_1)
 
         SLOTS = 2 * HEADS
@@ -308,10 +300,15 @@ def tile_ttcodegenattention_pa_t_kernel(
                     in_=staged_v[:, h0 : h0 + 2, j0:j1, :],
                 )
 
-            def passed_and_store(slot):
+            def passed(slot):
+                h, u = divmod(slot, 2)
+                copy_passed(
+                    b, g_first + u, h, staged_heads[h][:, :, u * GROUP : (u + 1) * GROUP, ROTARY:]
+                )
+
+            def store_head(slot):
                 h, u = divmod(slot, 2)
                 staged = staged_heads[h]
-                copy_passed(b, g_first + u, h, staged[:, :, u * GROUP : (u + 1) * GROUP, ROTARY:])
                 if u == 1:
                     for out, s in ((out_0, 0), (out_1, 1)):
                         nc.sync.dma_start(
@@ -330,6 +327,8 @@ def tile_ttcodegenattention_pa_t_kernel(
                         [P, 2, 2 * GROUP, HEAD_DIM], F32, name="staged_qk"
                     )
                 bank = multiply(psum_rot, b, g, qk_words[:, h, ROTATED, :], qk_planes[:, h, ROTATED, :])
+                if number > 0 or slot > 2:
+                    passed(slot)
                 prod = prod_pool.tile(full, F32)
                 nc.vector.tensor_tensor(
                     out=prod[:],
@@ -353,9 +352,11 @@ def tile_ttcodegenattention_pa_t_kernel(
                             if h_v % 2 == 1:
                                 store_values(h_v - 1, slot * GROUP, (slot + 1) * GROUP)
                     else:
-                        for earlier in range(2 if slot == 2 else 0):
-                            passed_and_store(earlier)
-                        passed_and_store(slot)
+                        for earlier in range(3 if slot == 2 else 0):
+                            passed(earlier)
+                            store_head(earlier)
+                        if slot > 2:
+                            store_head(slot)
                 else:
                     if slot < HEADS:
                         for u_v in range(2):
@@ -364,7 +365,7 @@ def tile_ttcodegenattention_pa_t_kernel(
                             )
                         if slot % 2 == 1:
                             store_values(slot - 1, 0, 2 * GROUP)
-                    passed_and_store(slot)
+                    store_head(slot)
                 if following and slot in (5, 6):
                     flipped_next = copy_flipped(flip_rows(following[0], following[1] + slot - 5))
                     if slot == 6:
@@ -375,11 +376,7 @@ def tile_ttcodegenattention_pa_t_kernel(
                 if number == 1:
                     if slot == 0:
                         tiles = angle_tiles()
-                    if slot < 4:
+                    if slot < 6:
                         angle_step(1, slot, tiles)
-                    if slot == 4:
-                        squared = half_angle_squares(tiles[2])
-                    if slot == 5:
-                        fill_table(nc.vector, 2, squared)
                     if slot == 7:
-                        fill_table(nc.vector, 3, squared)
+                        fill_table(1, tiles[2])

@@ -64,7 +64,8 @@ def tile_ttcodegenattention_pa_t_kernel(
                 ],
             )
 
-        load_x(0, 0, GROUP)
+        load_x(0, 0, GROUP // 2)
+        load_x(0, GROUP // 2, GROUP)
 
         w_words = consts.tile([P, 2 * 3 * EMBED], U8, align_bytes=64)
         nc.sync.dma_start(out=w_words[:].bitcast(I32), in_=w_qkv_words[0].bitcast(I32))
@@ -157,9 +158,8 @@ def tile_ttcodegenattention_pa_t_kernel(
         qk_words = consts.tile([P, HEADS, 2, 2 * HEAD_DIM], U8, align_bytes=64)
         qk_planes = consts.tile([P, HEADS, 2, HEAD_DIM], U8, align_bytes=64)
 
-        def regroup():
+        def regroup_words():
             words_in = w_words[:].rearrange("p (h t c) -> p h t c", h=HEADS, t=3)
-            planes_in = w_planes[:].rearrange("p (h t c) -> p h t c", h=HEADS, t=3)
             for s, t in enumerate((QUERY, KEY)):
                 for m in range(2):
                     first = 2 * ROTARY * s + ROTARY * m
@@ -171,12 +171,18 @@ def tile_ttcodegenattention_pa_t_kernel(
                             "p h (i m y) -> p h i m y", m=2, y=2
                         )[:, :, :, m, :],
                     )
+
+        def regroup_planes():
+            planes_in = w_planes[:].rearrange("p (h t c) -> p h t c", h=HEADS, t=3)
+            for s, t in enumerate((QUERY, KEY)):
                 nc.vector.tensor_copy(
                     out=qk_planes[:, :, ROTATED, ROTARY * s : ROTARY * (s + 1)].rearrange(
                         "p h (m i) -> p h m i", m=2
                     ),
                     in_=planes_in[:, :, t, 0:ROTARY].rearrange("p h (i m) -> p h m i", m=2),
                 )
+
+        def regroup_passed():
             for regrouped, raw, width in (
                 (qk_words, w_words, ROTARY // 2),
                 (qk_planes, w_planes, ROTARY // 4),
@@ -242,7 +248,7 @@ def tile_ttcodegenattention_pa_t_kernel(
                 )
             return bank
 
-        def copy_values(b, g, h, staged):
+        def copy_values(b, g, h, staged, copy):
             block = 3 * h + VALUE
             bank = multiply(
                 psum_copy,
@@ -251,7 +257,7 @@ def tile_ttcodegenattention_pa_t_kernel(
                 w_words[:, 2 * HEAD_DIM * block : 2 * HEAD_DIM * (block + 1)],
                 w_planes[:, HEAD_DIM * block : HEAD_DIM * (block + 1)],
             )
-            nc.scalar.copy(out=staged, in_=bank[:])
+            copy(out=staged, in_=bank[:])
 
         def copy_passed(b, g, h, staged):
             bank = multiply(psum_copy, b, g, qk_words[:, h, PASSED, :], qk_planes[:, h, PASSED, :])
@@ -277,10 +283,12 @@ def tile_ttcodegenattention_pa_t_kernel(
         banks_1 = flip_rows(0, 1)
         keep_busy(3)
         grouped_0 = copy_flipped(banks_0)
+        regroup_words()
+        quantise_rows(0, 0, grouped_0)
         fill_table(0, tiles[2])
         grouped_1 = copy_flipped(banks_1)
-        regroup()
-        quantise_rows(0, 0, grouped_0)
+        regroup_planes()
+        regroup_passed()
         quantise_rows(0, 1, grouped_1)
 
         SLOTS = 2 * HEADS
@@ -292,12 +300,12 @@ def tile_ttcodegenattention_pa_t_kernel(
             staged_heads = {}
             following = segments[number + 1] if number + 1 < len(segments) else None
 
-            def store_values(h0, j0, j1):
+            def store_values(h0, h1, j0, j1):
                 nc.sync.dma_start(
-                    out=out_2[b, h0 : h0 + 2].rearrange("h (c p r) d -> p h c r d", c=2, r=RUN)[
+                    out=out_2[b, h0:h1].rearrange("h (c p r) d -> p h c r d", c=2, r=RUN)[
                         :, :, j_first // RUN, j0:j1, :
                     ],
-                    in_=staged_v[:, h0 : h0 + 2, j0:j1, :],
+                    in_=staged_v[:, h0:h1, j0:j1, :],
                 )
 
             def passed(slot):
@@ -318,6 +326,14 @@ def tile_ttcodegenattention_pa_t_kernel(
                             in_=staged[:, s],
                         )
 
+            def first_values(u, h0, copies):
+                for h_v, copy in zip((h0, h0 + 1), copies):
+                    copy_values(
+                        b, g_first + u, h_v, staged_v[:, h_v, u * GROUP : (u + 1) * GROUP, :], copy
+                    )
+                store_values(h0, h0 + 2, u * GROUP, (u + 1) * GROUP)
+
+            on_scalar = (nc.scalar.copy, nc.scalar.copy)
             for slot in range(SLOTS):
                 h, u = divmod(slot, 2)
                 g = g_first + u
@@ -326,8 +342,13 @@ def tile_ttcodegenattention_pa_t_kernel(
                     staged_heads[h] = stage_qk_pool.tile(
                         [P, 2, 2 * GROUP, HEAD_DIM], F32, name="staged_qk"
                     )
+                if number == 0 and slot == 0:
+                    first_values(0, 0, on_scalar)
                 bank = multiply(psum_rot, b, g, qk_words[:, h, ROTATED, :], qk_planes[:, h, ROTATED, :])
-                if number > 0 or slot > 2:
+                if number == 0 and slot == 2:
+                    passed(0)
+                    passed(1)
+                if number > 0 or slot >= 2:
                     passed(slot)
                 prod = prod_pool.tile(full, F32)
                 nc.vector.tensor_tensor(
@@ -346,25 +367,26 @@ def tile_ttcodegenattention_pa_t_kernel(
                     op=ALU.add,
                 )
                 if number == 0:
-                    if slot < 2:
-                        for h_v in range(HEADS):
-                            copy_values(b, g_first + slot, h_v, staged_v[:, h_v, rows, :])
-                            if h_v % 2 == 1:
-                                store_values(h_v - 1, slot * GROUP, (slot + 1) * GROUP)
+                    if slot == 0:
+                        first_values(0, 2, on_scalar)
+                    elif slot == 1:
+                        first_values(1, 0, on_scalar)
+                        first_values(1, 2, (nc.vector.tensor_copy, nc.scalar.copy))
+                    elif slot == 2:
+                        store_head(1)
                     else:
-                        for earlier in range(3 if slot == 2 else 0):
-                            passed(earlier)
-                            store_head(earlier)
-                        if slot > 2:
-                            store_head(slot)
+                        store_head(slot)
                 else:
                     if slot < HEADS:
                         for u_v in range(2):
                             copy_values(
-                                b, g_first + u_v, slot, staged_v[:, slot, u_v * GROUP : (u_v + 1) * GROUP, :]
+                                b,
+                                g_first + u_v,
+                                slot,
+                                staged_v[:, slot, u_v * GROUP : (u_v + 1) * GROUP, :],
+                                nc.scalar.copy,
                             )
-                        if slot % 2 == 1:
-                            store_values(slot - 1, 0, 2 * GROUP)
+                        store_values(slot, slot + 1, 0, 2 * GROUP)
                     store_head(slot)
                 if following and slot in (5, 6):
                     flipped_next = copy_flipped(flip_rows(following[0], following[1] + slot - 5))

@@ -201,29 +201,34 @@ def tile_ttcodegenattention_pa_t_kernel(
             codes.append(quant_pool.tile([P, ROWS, P], U32, align_bytes=64, name="codes"))
             scales.append(quant_pool.tile([P, ROWS, P], U8, align_bytes=64, name="scales"))
 
-        def flip_rows(b, g):
+        def flip_pair(b, g, a0):
             x_words = x_tiles[b][:].bitcast(F32)
-            banks = []
-            for a0 in range(0, GROUP, 2):
-                flipped = psum_copy.tile([P, 2, 2, P], F32, tag="bank")
-                for a in range(2):
-                    for u in range(2):
-                        nc.tensor.transpose(
-                            flipped[:, a, u, :],
-                            x_words[:, g * GROUP + a0 + a, u : EMBED // 2 : 2],
-                            ident[:],
-                        )
-                banks.append(flipped)
-            return banks
+            flipped = psum_copy.tile([P, 2, 2, P], F32, tag="bank")
+            for a in range(2):
+                for u in range(2):
+                    nc.tensor.transpose(
+                        flipped[:, a, u, :],
+                        x_words[:, g * GROUP + a0 + a, u : EMBED // 2 : 2],
+                        ident[:],
+                    )
+            return flipped
 
-        def copy_flipped(banks):
-            grouped = grouped_pool.tile([P, GROUP, P, 4], BF16, align_bytes=64)
-            grouped_words = grouped[:].bitcast(F32)
+        def flip_rows(b, g):
+            return [flip_pair(b, g, a0) for a0 in range(0, GROUP, 2)]
+
+        def grouped_tile():
+            return grouped_pool.tile([P, GROUP, P, 4], BF16, align_bytes=64, name="grouped")
+
+        def copy_flipped(grouped, a0, flipped):
+            nc.scalar.copy(
+                out=grouped[:].bitcast(F32)[:, a0 : a0 + 2],
+                in_=flipped[:].rearrange("p a u r -> p a r u"),
+            )
+
+        def copy_group(banks):
+            grouped = grouped_tile()
             for a0, flipped in zip(range(0, GROUP, 2), banks):
-                nc.scalar.copy(
-                    out=grouped_words[:, a0 : a0 + 2],
-                    in_=flipped[:].rearrange("p a u r -> p a r u"),
-                )
+                copy_flipped(grouped, a0, flipped)
             return grouped
 
         def quantise_rows(b, g, grouped):
@@ -282,11 +287,11 @@ def tile_ttcodegenattention_pa_t_kernel(
         keep_busy(2)
         banks_1 = flip_rows(0, 1)
         keep_busy(3)
-        grouped_0 = copy_flipped(banks_0)
+        grouped_0 = copy_group(banks_0)
         regroup_words()
         quantise_rows(0, 0, grouped_0)
         fill_table(0, tiles[2])
-        grouped_1 = copy_flipped(banks_1)
+        grouped_1 = copy_group(banks_1)
         regroup_planes()
         regroup_passed()
         quantise_rows(0, 1, grouped_1)
@@ -298,6 +303,7 @@ def tile_ttcodegenattention_pa_t_kernel(
             j_first = g_first * GROUP
             staged_v = stage_v_pool.tile([P, HEADS, 2 * GROUP, HEAD_DIM], F32)
             staged_heads = {}
+            grouped_next = []
             following = segments[number + 1] if number + 1 < len(segments) else None
 
             def store_values(h0, h1, j0, j1):
@@ -314,17 +320,14 @@ def tile_ttcodegenattention_pa_t_kernel(
                     b, g_first + u, h, staged_heads[h][:, :, u * GROUP : (u + 1) * GROUP, ROTARY:]
                 )
 
-            def store_head(slot):
-                h, u = divmod(slot, 2)
-                staged = staged_heads[h]
-                if u == 1:
-                    for out, s in ((out_0, 0), (out_1, 1)):
-                        nc.sync.dma_start(
-                            out=out[b, h].rearrange("(c p r) d -> p c r d", c=2, r=RUN)[
-                                :, j_first // RUN, :, :
-                            ],
-                            in_=staged[:, s],
-                        )
+            def store_head(h, j0, j1):
+                for out, s in ((out_0, 0), (out_1, 1)):
+                    nc.sync.dma_start(
+                        out=out[b, h].rearrange("(c p r) d -> p c r d", c=2, r=RUN)[
+                            :, j_first // RUN, j0:j1, :
+                        ],
+                        in_=staged_heads[h][:, s, j0:j1],
+                    )
 
             def first_values(u, h0, copies):
                 for h_v, copy in zip((h0, h0 + 1), copies):
@@ -345,6 +348,15 @@ def tile_ttcodegenattention_pa_t_kernel(
                 if number == 0 and slot == 0:
                     first_values(0, 0, on_scalar)
                 bank = multiply(psum_rot, b, g, qk_words[:, h, ROTATED, :], qk_planes[:, h, ROTATED, :])
+                if following and 3 <= slot <= 6:
+                    ahead, pair = divmod(slot - 3, 2)
+                    if pair == 0:
+                        grouped_next.append(grouped_tile())
+                    copy_flipped(
+                        grouped_next[ahead],
+                        2 * pair,
+                        flip_pair(following[0], following[1] + ahead, 2 * pair),
+                    )
                 if number == 0 and slot == 2:
                     passed(0)
                     passed(1)
@@ -366,6 +378,8 @@ def tile_ttcodegenattention_pa_t_kernel(
                     in1=prod[:, :, :, PAIRS:, :].rearrange("p a s i e -> p a s (i e)"),
                     op=ALU.add,
                 )
+                if following and slot >= 6:
+                    quantise_rows(following[0], following[1] + slot - 6, grouped_next[slot - 6])
                 if number == 0:
                     if slot == 0:
                         first_values(0, 2, on_scalar)
@@ -373,9 +387,11 @@ def tile_ttcodegenattention_pa_t_kernel(
                         first_values(1, 0, on_scalar)
                         first_values(1, 2, (nc.vector.tensor_copy, nc.scalar.copy))
                     elif slot == 2:
-                        store_head(1)
-                    else:
-                        store_head(slot)
+                        store_head(0, 0, 2 * GROUP)
+                    elif slot >= SLOTS - 2:
+                        store_head(h, u * GROUP, (u + 1) * GROUP)
+                    elif u == 1:
+                        store_head(h, 0, 2 * GROUP)
                 else:
                     if slot < HEADS:
                         for u_v in range(2):
@@ -387,14 +403,8 @@ def tile_ttcodegenattention_pa_t_kernel(
                                 nc.scalar.copy,
                             )
                         store_values(slot, slot + 1, 0, 2 * GROUP)
-                    store_head(slot)
-                if following and slot in (5, 6):
-                    flipped_next = copy_flipped(flip_rows(following[0], following[1] + slot - 5))
-                    if slot == 6:
-                        quantise_rows(following[0], following[1], waiting)
-                    waiting = flipped_next
-                if following and slot == 7:
-                    quantise_rows(following[0], following[1] + 1, waiting)
+                    if u == 1:
+                        store_head(h, 0, 2 * GROUP)
                 if number == 1:
                     if slot == 0:
                         tiles = angle_tiles()

import math
from contextlib import ExitStack

import concourse.mybir as mybir
from concourse.masks import make_identity

F32 = mybir.dt.float32
BF16 = mybir.dt.bfloat16
I32 = mybir.dt.int32
U32 = mybir.dt.uint32
U8 = mybir.dt.uint8
FP8X4 = mybir.dt.float8_e4m3fn_x4
FP4X4 = mybir.dt.float4_e2m1fn_x4
ALU = mybir.AluOpType
FUNC = mybir.ActivationFunctionType

P = 128
BATCH, SEQ, EMBED = 2, 2048, 512
HEADS, HEAD_DIM, ROTARY = 4, 128, 64
PAIRS = ROTARY // 2
ROPE_BASE = 10000.0

ROWS = SEQ // P
RUN = ROWS // 2
GROUP = 4
GROUPS = ROWS // GROUP
QUERY, VALUE, KEY = 0, 1, 2
ROTATED, PASSED = 0, 1

ROUND = 1.5 * 2.0**23

FLOPS = 2 * BATCH * SEQ * EMBED * 3 * EMBED


def tile_ttcodegenattention_pa_t_kernel(
    tc, hidden_states, w_qkv_words, w_qkv_scales, out_0, out_1, out_2
):
    nc = tc.nc
    with ExitStack() as ctx:
        consts = ctx.enter_context(tc.tile_pool(name="consts", bufs=1))
        angle_pool = ctx.enter_context(tc.tile_pool(name="angles", bufs=2))
        x_pool = ctx.enter_context(tc.tile_pool(name="x", bufs=BATCH))
        grouped_pool = ctx.enter_context(tc.tile_pool(name="grouped", bufs=2))
        quant_pool = ctx.enter_context(tc.tile_pool(name="quant", bufs=BATCH))
        prod_pool = ctx.enter_context(tc.tile_pool(name="prod", bufs=3))
        stage_v_pool = ctx.enter_context(tc.tile_pool(name="stage_v", bufs=3))
        stage_qk_pool = ctx.enter_context(tc.tile_pool(name="stage_qk", bufs=8))
        psum_rot = ctx.enter_context(tc.psum_pool(name="psum_rot", bufs=2))
        psum_copy = ctx.enter_context(tc.psum_pool(name="psum_copy", bufs=6))
        ctx.enter_context(tc.manual_schedule())

        zeros = consts.tile([P, 4 * P], BF16)
        nc.gpsimd.memset(zeros[:], 0.0)

        x_tiles = []
        for b in range(BATCH):
            x_tiles.append(x_pool.tile([P, ROWS, EMBED], BF16, name="x_rows"))

        def load_x(b, j0, j1):
            nc.sync.dma_start(
                out=x_tiles[b][:, j0:j1, :],
                in_=hidden_states[b].rearrange("(c p r) k -> p c r k", c=2, r=RUN)[
                    :, j0 // RUN, j0 % RUN : j0 % RUN + j1 - j0, :
                ],
            )

        load_x(0, 0, GROUP // 2)
        load_x(0, GROUP // 2, GROUP)

        w_words = consts.tile([P, 2 * 3 * EMBED], U8, align_bytes=64)
        nc.sync.dma_start(out=w_words[:].bitcast(I32), in_=w_qkv_words[0].bitcast(I32))
        w_planes = consts.tile([P, 3 * EMBED], U8, align_bytes=64)
        nc.vector.memset(w_planes[:].bitcast(I32), 0)
        scale_rows = w_qkv_scales[0].bitcast(I32)
        for quadrant in range(4):
            nc.sync.dma_start(
                out=w_planes[32 * quadrant : 32 * quadrant + 4, :].bitcast(I32),
                in_=scale_rows[4 * quadrant : 4 * quadrant + 4, :],
            )
        load_x(0, GROUP, 2 * GROUP)
        load_x(1, 0, 2 * GROUP)
        load_x(0, 2 * GROUP, ROWS)
        load_x(1, 2 * GROUP, ROWS)

        warm = consts.tile([P, 2], F32)
        nc.gpsimd.memset(warm[:], 0.0)
        nc.scalar.activation(out=warm[:, 1:2], in_=warm[:, 0:1], func=FUNC.Sin)
        position = consts.tile([P, ROWS], F32)
        nc.gpsimd.iota(
            position[:],
            pattern=[[SEQ // 2, 2], [1, RUN]],
            base=0,
            channel_multiplier=RUN,
            allow_small_or_imprecise_dtypes=True,
        )
        ident = consts.tile([P, P], F32)
        make_identity(nc, ident[:])
        ratio = ROPE_BASE ** (-1.0 / PAIRS)
        frequency = consts.tile([P, PAIRS], F32)
        nc.vector.memset(frequency[:, 0:1], 1.0)
        filled = 1
        while filled < PAIRS:
            nc.vector.tensor_scalar_mul(
                out=frequency[:, filled : 2 * filled],
                in0=frequency[:, 0:filled],
                scalar1=ratio**filled,
            )
            filled *= 2

        table = consts.tile([P, ROWS, 2, PAIRS, 2], F32)
        HALF = ROWS // 2
        shape = [P, HALF, PAIRS]

        def angle_tiles():
            turns = angle_pool.tile(shape, F32)
            whole = angle_pool.tile(shape, F32)
            parts = angle_pool.tile([P, 3, HALF, PAIRS], F32)
            return turns, whole, parts

        def angle_step(c, step, tiles):
            turns, whole, parts = tiles
            if step == 0:
                nc.vector.scalar_tensor_tensor(
                    out=turns[:],
                    in0=position[:, c * HALF : (c + 1) * HALF].unsqueeze(2).to_broadcast(shape),
                    scalar=1.0 / (2.0 * math.pi),
                    in1=frequency[:].unsqueeze(1).to_broadcast(shape),
                    op0=ALU.mult,
                    op1=ALU.mult,
                )
            elif step == 1:
                nc.vector.tensor_scalar_add(out=whole[:], in0=turns[:], scalar1=ROUND)
            elif step == 2:
                nc.vector.scalar_tensor_tensor(
                    out=parts[:, 0],
                    in0=whole[:],
                    scalar=ROUND,
                    in1=turns[:],
                    op0=ALU.subtract,
                    op1=ALU.subtract,
                )
            elif step == 3:
                nc.vector.tensor_scalar_mul(out=parts[:, 2], in0=parts[:, 0], scalar1=-1.0)
            elif step == 4:
                nc.vector.tensor_tensor(out=parts[:, 1], in0=parts[:, 0], in1=parts[:, 2], op=ALU.min)
            else:
                nc.vector.tensor_scalar_add(out=parts[:, 1], in0=parts[:, 1], scalar1=0.25)

        def fill_table(c, parts):
            for m in range(2):
                nc.scalar.activation(
                    out=table[:, c * HALF : (c + 1) * HALF, m],
                    in_=parts[:, 1 - m : 3 - m].rearrange("p e r i -> p r i e"),
                    func=FUNC.Sin,
                    scale=2.0 * math.pi,
                )

        qk_words = consts.tile([P, HEADS, 2, 2 * HEAD_DIM], U8, align_bytes=64)
        qk_planes = consts.tile([P, HEADS, 2, HEAD_DIM], U8, align_bytes=64)

        def regroup_words():
            words_in = w_words[:].rearrange("p (h t c) -> p h t c", h=HEADS, t=3)
            for s, t in enumerate((QUERY, KEY)):
                for m in range(2):
                    first = 2 * ROTARY * s + ROTARY * m
                    nc.vector.tensor_copy(
                        out=qk_words[:, :, ROTATED, first : first + ROTARY].rearrange(
                            "p h (i y) -> p h i y", y=2
                        ),
                        in_=words_in[:, :, t, 0 : 2 * ROTARY].rearrange(
                            "p h (i m y) -> p h i m y", m=2, y=2
                        )[:, :, :, m, :],
                    )

        def regroup_planes():
            planes_in = w_planes[:].rearrange("p (h t c) -> p h t c", h=HEADS, t=3)
            for s, t in enumerate((QUERY, KEY)):
                nc.vector.tensor_copy(
                    out=qk_planes[:, :, ROTATED, ROTARY * s : ROTARY * (s + 1)].rearrange(
                        "p h (m i) -> p h m i", m=2
                    ),
                    in_=planes_in[:, :, t, 0:ROTARY].rearrange("p h (i m) -> p h m i", m=2),
                )

        def regroup_passed():
            for regrouped, raw, width in (
                (qk_words, w_words, ROTARY // 2),
                (qk_planes, w_planes, ROTARY // 4),
            ):
                nc.vector.tensor_copy(
                    out=regrouped[:].bitcast(I32)[:, :, PASSED, :].rearrange(
                        "p h (s c) -> p h s c", s=2
                    ),
                    in_=raw[:].bitcast(I32).rearrange("p (h t c) -> p h t c", h=HEADS, t=3)[
                        :, :, QUERY : KEY + 1 : 2, width : 2 * width
                    ],
                )

        codes, scales = [], []
        for b in range(BATCH):
            codes.append(quant_pool.tile([P, ROWS, P], U32, align_bytes=64, name="codes"))
            scales.append(quant_pool.tile([P, ROWS, P], U8, align_bytes=64, name="scales"))

        def flip_pair(b, g, a0):
            x_words = x_tiles[b][:].bitcast(F32)
            flipped = psum_copy.tile([P, 2, 2, P], F32, tag="bank")
            for a in range(2):
                for u in range(2):
                    nc.tensor.transpose(
                        flipped[:, a, u, :],
                        x_words[:, g * GROUP + a0 + a, u : EMBED // 2 : 2],
                        ident[:],
                    )
            return flipped

        def flip_rows(b, g):
            return [flip_pair(b, g, a0) for a0 in range(0, GROUP, 2)]

        def grouped_tile():
            return grouped_pool.tile([P, GROUP, P, 4], BF16, align_bytes=64, name="grouped")

        def copy_flipped(grouped, a0, flipped):
            nc.scalar.copy(
                out=grouped[:].bitcast(F32)[:, a0 : a0 + 2],
                in_=flipped[:].rearrange("p a u r -> p a r u"),
            )

        def copy_group(banks):
            grouped = grouped_tile()
            for a0, flipped in zip(range(0, GROUP, 2), banks):
                copy_flipped(grouped, a0, flipped)
            return grouped

        def quantise_rows(b, g, grouped):
            rows = slice(g * GROUP, (g + 1) * GROUP)
            nc.vector.quantize_mx(
                out=codes[b][:, rows].rearrange("p j r -> p (j r)").bitcast(FP8X4),
                scales=scales[b][:, rows].rearrange("p j r -> p (j r)"),
                in_=grouped[:].rearrange("p j r t -> p (j r t)"),
            )

        def multiply(pool, b, g, words, planes):
            bank = pool.tile([P, GROUP, HEAD_DIM], F32, tag="bank")
            for a in range(GROUP):
                nc.tensor.matmul_mx(
                    out=bank[:, a, :],
                    lhsT=codes[b][:, g * GROUP + a, :].bitcast(FP8X4),
                    lhsT_scale=scales[b][:, g * GROUP + a, :],
                    rhs=words.bitcast(FP4X4),
                    rhs_scale=planes,
                    start=True,
                    stop=True,
                )
            return bank

        def copy_values(b, g, h, staged, copy):
            block = 3 * h + VALUE
            bank = multiply(
                psum_copy,
                b,
                g,
                w_words[:, 2 * HEAD_DIM * block : 2 * HEAD_DIM * (block + 1)],
                w_planes[:, HEAD_DIM * block : HEAD_DIM * (block + 1)],
            )
            copy(out=staged, in_=bank[:])

        def copy_passed(b, g, h, staged):
            bank = multiply(psum_copy, b, g, qk_words[:, h, PASSED, :], qk_planes[:, h, PASSED, :])
            nc.scalar.copy(
                out=staged.rearrange("p s a d -> p a s d"),
                in_=bank[:].rearrange("p a (s d) -> p a s d", s=2),
            )

        idle_bank = psum_copy.tile([P, 4 * P], F32, tag="bank")

        def keep_busy(count):
            for n in range(count):
                nc.tensor.matmul(
                    idle_bank[:], lhsT=zeros[:, 0:P], rhs=zeros[:], start=True, stop=True
                )

        tiles = angle_tiles()
        for step in range(6):
            angle_step(0, step, tiles)
        keep_busy(5)
        banks_0 = flip_rows(0, 0)
        keep_busy(2)
        banks_1 = flip_rows(0, 1)
        keep_busy(3)
        grouped_0 = copy_group(banks_0)
        regroup_words()
        quantise_rows(0, 0, grouped_0)
        fill_table(0, tiles[2])
        grouped_1 = copy_group(banks_1)
        regroup_planes()
        regroup_passed()
        quantise_rows(0, 1, grouped_1)

        SLOTS = 2 * HEADS
        segments = ((0, 0), (1, 0), (0, 2), (1, 2))
        full = [P, GROUP, 2, ROTARY, 2]
        for number, (b, g_first) in enumerate(segments):
            j_first = g_first * GROUP
            staged_v = stage_v_pool.tile([P, HEADS, 2 * GROUP, HEAD_DIM], F32)
            staged_heads = {}
            grouped_next = []
            following = segments[number + 1] if number + 1 < len(segments) else None

            def store_values(h0, h1, j0, j1):
                nc.sync.dma_start(
                    out=out_2[b, h0:h1].rearrange("h (c p r) d -> p h c r d", c=2, r=RUN)[
                        :, :, j_first // RUN, j0:j1, :
                    ],
                    in_=staged_v[:, h0:h1, j0:j1, :],
                )

            def passed(slot):
                h, u = divmod(slot, 2)
                copy_passed(
                    b, g_first + u, h, staged_heads[h][:, :, u * GROUP : (u + 1) * GROUP, ROTARY:]
                )

            def store_head(h, j0, j1):
                for out, s in ((out_0, 0), (out_1, 1)):
                    nc.sync.dma_start(
                        out=out[b, h].rearrange("(c p r) d -> p c r d", c=2, r=RUN)[
                            :, j_first // RUN, j0:j1, :
                        ],
                        in_=staged_heads[h][:, s, j0:j1],
                    )

            def first_values(u, h0, copies):
                for h_v, copy in zip((h0, h0 + 1), copies):
                    copy_values(
                        b, g_first + u, h_v, staged_v[:, h_v, u * GROUP : (u + 1) * GROUP, :], copy
                    )
                store_values(h0, h0 + 2, u * GROUP, (u + 1) * GROUP)

            on_scalar = (nc.scalar.copy, nc.scalar.copy)
            for slot in range(SLOTS):
                h, u = divmod(slot, 2)
                g = g_first + u
                rows = slice(u * GROUP, (u + 1) * GROUP)
                if u == 0:
                    staged_heads[h] = stage_qk_pool.tile(
                        [P, 2, 2 * GROUP, HEAD_DIM], F32, name="staged_qk"
                    )
                if number == 0 and slot == 0:
                    first_values(0, 0, on_scalar)
                bank = multiply(psum_rot, b, g, qk_words[:, h, ROTATED, :], qk_planes[:, h, ROTATED, :])
                if following and 3 <= slot <= 6:
                    ahead, pair = divmod(slot - 3, 2)
                    if pair == 0:
                        grouped_next.append(grouped_tile())
                    copy_flipped(
                        grouped_next[ahead],
                        2 * pair,
                        flip_pair(following[0], following[1] + ahead, 2 * pair),
                    )
                if number == 0 and slot == 2:
                    passed(0)
                    passed(1)
                if number > 0 or slot >= 2:
                    passed(slot)
                prod = prod_pool.tile(full, F32)
                nc.vector.tensor_tensor(
                    out=prod[:],
                    in0=bank[:].rearrange("p a (s c) -> p a s c", s=2).unsqueeze(4).to_broadcast(full),
                    in1=table[:, g * GROUP : (g + 1) * GROUP]
                    .rearrange("p a m i e -> p a (m i) e")
                    .unsqueeze(2)
                    .to_broadcast(full),
                    op=ALU.mult,
                )
                nc.gpsimd.tensor_tensor(
                    out=staged_heads[h][:, :, rows, 0:ROTARY].rearrange("p s a d -> p a s d"),
                    in0=prod[:, :, :, 0:PAIRS, :].rearrange("p a s i e -> p a s (i e)"),
                    in1=prod[:, :, :, PAIRS:, :].rearrange("p a s i e -> p a s (i e)"),
                    op=ALU.add,
                )
                if following and slot >= 6:
                    quantise_rows(following[0], following[1] + slot - 6, grouped_next[slot - 6])
                if number == 0:
                    if slot == 0:
                        first_values(0, 2, on_scalar)
                    elif slot == 1:
                        first_values(1, 0, on_scalar)
                        first_values(1, 2, (nc.vector.tensor_copy, nc.scalar.copy))
                    elif slot == 2:
                        store_head(0, 0, 2 * GROUP)
                    elif slot >= SLOTS - 2:
                        store_head(h, u * GROUP, (u + 1) * GROUP)
                    elif u == 1:
                        store_head(h, 0, 2 * GROUP)
                else:
                    if slot < HEADS:
                        for u_v in range(2):
                            copy_values(
                                b,
                                g_first + u_v,
                                slot,
                                staged_v[:, slot, u_v * GROUP : (u_v + 1) * GROUP, :],
                                nc.scalar.copy,
                            )
                        store_values(slot, slot + 1, 0, 2 * GROUP)
                    if u == 1:
                        store_head(h, 0, 2 * GROUP)
                if number == 1:
                    if slot == 0:
                        tiles = angle_tiles()
                    if slot < 6:
                        angle_step(1, slot, tiles)
                    if slot == 7:
                        fill_table(1, tiles[2])
